import numpy as np
import ml_dtypes


def mxq(x, axis, fmt="e4m3"):
    dtype, down = {"e4m3": (ml_dtypes.float8_e4m3fn, 7), "e5m2": (ml_dtypes.float8_e5m2, 14)}[fmt]
    v = np.moveaxis(np.asarray(x, np.float32).astype(ml_dtypes.bfloat16).astype(np.float64), axis, -1)
    blocks = v.reshape(v.shape[:-1] + (-1, 32))
    amax = np.abs(blocks).max(-1, keepdims=True)
    byte = np.maximum(np.where(amax > 0, np.frexp(amax)[1] - 1 + 127, 0) - down, 1)
    scale = np.exp2(byte - 127.0)
    codes = (blocks / scale).astype(np.float32).astype(dtype).astype(np.float64)
    return np.moveaxis((codes * scale).reshape(v.shape), -1, axis)


WIDE = False


def mx_kscale(k):
    if not WIDE:
        return np.ones(k)
    levels = np.array([10, -10, 5, -5, 0])
    if k % 512:
        return np.exp2(np.random.permutation(np.resize(levels, k // 32))).repeat(32)
    a = np.empty((k // 512, 16))
    for p in range(k // 512):
        a[p, :8] = np.random.permutation(np.resize(levels, 8))
        for g in range(8):
            far = levels[np.abs(levels - a[p, g]) >= 10]
            a[p, g + 8] = far[np.random.randint(len(far))]
    return np.exp2(a.ravel()).repeat(32)


BF16 = ml_dtypes.bfloat16


def bf(x):
    return np.asarray(x, np.float32).astype(BF16)


def f64(x):
    return np.asarray(x).astype(np.float64)


B, IN, H = 4096, 512, 512


def sigmoid(v):
    return 1.0 / (1.0 + np.exp(-v))


def setup_inputs():
    s, t = mx_kscale(IN), mx_kscale(H)
    a = np.sqrt(2.0 / (IN + H))
    return {
        "x": bf(np.random.standard_normal((B, IN)) * s),
        "h_prev": bf(np.random.standard_normal((B, H)) * t),
        "m_prev": bf(np.random.standard_normal((B, H)) * 0.5),
        "Wi_x": bf(np.random.standard_normal((H, IN)) * a / s),
        "b_i": bf(np.random.standard_normal(H) * 0.3),
        "Wi_h": bf(np.random.standard_normal((H, H)) * a / t),
        "Wf_x": bf(np.random.standard_normal((H, IN)) * a / s),
        "b_f": bf(2.0 + np.random.standard_normal(H) * 0.3),
        "Wf_h": bf(np.random.standard_normal((H, H)) * a / t),
    }


def reference(x, h_prev, m_prev, Wi_x, b_i, Wi_h, Wf_x, b_f, Wf_h):
    xq = mxq(f64(x), 1, "e4m3")
    hq = mxq(f64(h_prev), 1, "e4m3")
    i_tilde = (xq @ mxq(f64(Wi_x), 1, "e4m3").T) + f64(b_i) + (hq @ mxq(f64(Wi_h), 1, "e4m3").T)
    f_aff = (xq @ mxq(f64(Wf_x), 1, "e4m3").T) + f64(b_f) + (hq @ mxq(f64(Wf_h), 1, "e4m3").T)
    log_f = np.log(np.maximum(sigmoid(f_aff), 1e-8))
    m_t = np.maximum(log_f + f64(m_prev), i_tilde)
    i_prime = np.exp(i_tilde - m_t)
    f_prime = np.exp(log_f + f64(m_prev) - m_t)
    return m_t, i_prime, f_prime

@@ -1,0 +1,324 @@
+from contextlib import ExitStack
+
+import concourse.mybir as mybir
+from concourse.masks import make_identity
+
+F32 = mybir.dt.float32
+BF16 = mybir.dt.bfloat16
+U32 = mybir.dt.uint32
+U8 = mybir.dt.uint8
+FP8X4 = mybir.dt.float8_e4m3fn_x4
+ACT = mybir.ActivationFunctionType
+ALU = mybir.AluOpType
+
+P = 128
+BATCH = 4096
+FEAT = 512
+HID = 512
+WORDS = FEAT // 2
+CHUNKS = HID // P
+
+PAIR_TILES = 2
+PAIR_ROWS = PAIR_TILES * P
+GROUP_PAIRS = 2
+GROUP_TILES = GROUP_PAIRS * PAIR_TILES
+GROUP_ROWS = GROUP_TILES * P
+ROUND_GROUPS = 2
+ROUND_PAIRS = ROUND_GROUPS * GROUP_PAIRS
+N_GROUPS = BATCH // GROUP_ROWS
+N_ROUNDS = N_GROUPS // ROUND_GROUPS
+N_PAIRS = BATCH // PAIR_ROWS
+assert ROUND_GROUPS == 2
+
+E_MAX = 1.0e8 - 1.0
+
+FLOPS = 2 * BATCH * HID * FEAT * 4
+
+
+def tile_slstmlayer_pa_t_kernel(
+    tc, x, h_prev, m_prev, Wi_x, b_i, Wi_h, Wf_x, b_f, Wf_h, out_0, out_1, out_2
+):
+    nc = tc.nc
+    with ExitStack() as ctx:
+        consts = ctx.enter_context(tc.tile_pool(name="consts", bufs=1))
+        raws = ctx.enter_context(tc.tile_pool(name="raws", bufs=4 * ROUND_GROUPS))
+        m_pool = ctx.enter_context(tc.tile_pool(name="m_pool", bufs=2 * ROUND_GROUPS))
+        grouped_pool = ctx.enter_context(tc.tile_pool(name="grouped_pool", bufs=2))
+        codes_pool = ctx.enter_context(tc.tile_pool(name="codes_pool", bufs=3 * ROUND_GROUPS))
+        gate_pool = ctx.enter_context(tc.tile_pool(name="gate_pool", bufs=2 * ROUND_GROUPS))
+        arg_pool = ctx.enter_context(tc.tile_pool(name="arg_pool", bufs=ROUND_PAIRS + 3))
+        m_t_pool = ctx.enter_context(tc.tile_pool(name="m_t_pool", bufs=4))
+        psum = ctx.enter_context(tc.psum_pool(name="psum", bufs=2))
+        ctx.enter_context(tc.manual_schedule())
+
+        ident_f32 = consts.tile([P, P], F32, tag="ident_f32")
+        make_identity(nc, ident_f32[:])
+        ident_bf16 = consts.tile([P, P], BF16, tag="ident_bf16")
+        make_identity(nc, ident_bf16[:])
+
+        def pair_rows(dram, s):
+            rows = dram[s * PAIR_ROWS : (s + 1) * PAIR_ROWS, :]
+            return rows.rearrange("(p t) k -> p (t k)", t=PAIR_TILES)
+
+        def load_group(rows_tile, dram, g):
+            rows = dram[g * GROUP_ROWS : (g + 1) * GROUP_ROWS, :]
+            nc.sync.dma_start(
+                out=rows_tile[:].rearrange("p (a w) -> p a w", a=GROUP_PAIRS),
+                in_=rows.rearrange("(a p t) k -> p a (t k)", a=GROUP_PAIRS, t=PAIR_TILES),
+            )
+
+        def load_weight(w):
+            raw = raws.tile([P, GROUP_TILES * FEAT], BF16, tag="w_raw", bufs=2)
+            nc.sync.dma_start(
+                out=raw[:].rearrange("p (c k) -> p c k", c=CHUNKS),
+                in_=w.rearrange("(c p) k -> p c k", p=P),
+            )
+            return raw
+
+        x_raw = {}
+        h_raw = {}
+        m_rows = {}
+
+        def round_groups(k):
+            return range(k * ROUND_GROUPS, (k + 1) * ROUND_GROUPS) if k < N_ROUNDS else ()
+
+        def load_group_activations(g):
+            x_raw[g] = raws.tile([P, GROUP_TILES * FEAT], BF16, tag="raw", name="x_raw")
+            load_group(x_raw[g], x, g)
+            h_raw[g] = raws.tile([P, GROUP_TILES * FEAT], BF16, tag="raw", name="h_raw")
+            load_group(h_raw[g], h_prev, g)
+
+        def load_activations(k):
+            for g in round_groups(k):
+                load_group_activations(g)
+
+        def load_m_prev(k):
+            for g in round_groups(k):
+                m_rows[g] = m_pool.tile([P, GROUP_TILES * HID], BF16, tag="m", name="m_rows")
+                load_group(m_rows[g], m_prev, g)
+
+        def new_operand(raw, pool, name, side):
+            grouped = grouped_pool.tile([P, 4 * GROUP_ROWS], BF16, tag=side + "_grouped", align_bytes=64)
+            codes = pool.tile([P, GROUP_ROWS], U32, tag=name + "_codes", align_bytes=64)
+            scales = pool.tile([P, GROUP_ROWS], U8, tag=name + "_scales", align_bytes=64)
+            return {"raw": raw, "grouped": grouped, "codes": codes, "scales": scales}
+
+        def transpose_half(operand, half, bank_tag):
+            words = operand["raw"][:].bitcast(F32)
+            bank = psum.tile([P, 2, PAIR_ROWS], F32, tag=bank_tag)
+            for t in range(PAIR_TILES):
+                for u in range(2):
+                    row = (half * PAIR_TILES + t) * WORDS
+                    nc.tensor.transpose(
+                        bank[:, u, t * P : (t + 1) * P], words[:, row + u : row + WORDS : 2], ident_f32[:]
+                    )
+            return bank
+
+        def copy_out_half(operand, half, bank, copy):
+            words = operand["grouped"][:].bitcast(F32)[:, half * 2 * PAIR_ROWS : (half + 1) * 2 * PAIR_ROWS]
+            copy(out=words.rearrange("p (r u) -> p r u", u=2), in_=bank[:].rearrange("p u r -> p r u"))
+
+        def quantise(operand):
+            nc.vector.quantize_mx(
+                out=operand["codes"][:].bitcast(FP8X4), scales=operand["scales"][:], in_=operand["grouped"][:]
+            )
+
+        def prepare_weight(raw, name, side, second_copy):
+            operand = new_operand(raw, consts, name, side)
+            copy_out_half(operand, 0, transpose_half(operand, 0, "pi"), nc.vector.tensor_copy)
+            copy_out_half(operand, 1, transpose_half(operand, 1, "pi"), second_copy)
+            quantise(operand)
+            return operand
+
+        def mx_product(out, stationary, stationary_cols, moving, start, stop):
+            nc.tensor.matmul_mx(
+                out=out,
+                lhsT=stationary["codes"][:, stationary_cols].bitcast(FP8X4),
+                lhsT_scale=stationary["scales"][:, stationary_cols],
+                rhs=moving["codes"][:].bitcast(FP8X4),
+                rhs_scale=moving["scales"][:],
+                start=start,
+                stop=stop,
+            )
+
+        weights = {}
+        x_ops = {}
+        h_ops = {}
+        gates = {}
+        word_banks = {}
+        banks = {}
+        pair_args = {}
+
+        def forget_gate(g):
+            gates[g] = gate_pool.tile([P, CHUNKS, GROUP_ROWS], F32, tag="gate", name="gate")
+            for c in range(CHUNKS):
+                f_bank = psum.tile([P, GROUP_ROWS], F32, tag="pf")
+                chunk_cols = slice(c * P, (c + 1) * P)
+                mx_product(f_bank[:], weights["fx"], chunk_cols, x_ops[g], True, False)
+                mx_product(f_bank[:], weights["fh"], chunk_cols, h_ops[g], False, True)
+                nc.scalar.activation(
+                    out=gates[g][:, c, :], in_=f_bank[:], func=ACT.Exp,
+                    bias=neg_bf[:, c : c + 1], scale=-1.0,
+                )
+                nc.gpsimd.tensor_scalar(
+                    out=gates[g][:, c, :], in0=gates[g][:, c, :],
+                    scalar1=E_MAX, scalar2=0.0, op0=ALU.min, op1=ALU.max,
+                )
+
+        def logarithms(k):
+            for g in round_groups(k):
+                flat = gates[g][:].rearrange("p c b -> p (c b)")
+                nc.scalar.activation(out=flat, in_=flat, func=ACT.Ln, bias=one[:], scale=1.0)
+
+        def start_group(g, bank_tag):
+            x_ops[g] = new_operand(x_raw[g], codes_pool, "x", "x")
+            h_ops[g] = new_operand(h_raw[g], codes_pool, "h", "h")
+            word_banks[g] = (transpose_half(x_ops[g], 0, bank_tag), transpose_half(h_ops[g], 0, bank_tag))
+
+        def middle_group(g, h_copy):
+            x_bank, h_bank = word_banks[g]
+            copy_out_half(x_ops[g], 0, x_bank, nc.vector.tensor_copy)
+            copy_out_half(h_ops[g], 0, h_bank, h_copy)
+            word_banks[g] = (transpose_half(x_ops[g], 1, "tr"), transpose_half(h_ops[g], 1, "tr"))
+
+        def finish_group(g, h_copy):
+            x_bank, h_bank = word_banks[g]
+            copy_out_half(x_ops[g], 1, x_bank, nc.vector.tensor_copy)
+            copy_out_half(h_ops[g], 1, h_bank, h_copy)
+            quantise(x_ops[g])
+            quantise(h_ops[g])
+
+        def prepare_group(g, h_copy):
+            start_group(g, "tr")
+            middle_group(g, h_copy)
+            finish_group(g, h_copy)
+
+        def chain_banks(s):
+            g, half = divmod(s, GROUP_PAIRS)
+            i_banks = []
+            for t in range(PAIR_TILES):
+                j = half * PAIR_TILES + t
+                i_bank = psum.tile([P, HID], F32, tag="pi")
+                tile_cols = slice(j * P, (j + 1) * P)
+                mx_product(i_bank[:], x_ops[g], tile_cols, weights["ix"], True, False)
+                mx_product(i_bank[:], h_ops[g], tile_cols, weights["ih"], False, True)
+                i_banks.append(i_bank)
+            sum_banks = []
+            for t in range(PAIR_TILES):
+                j = half * PAIR_TILES + t
+                sum_bank = psum.tile([P, HID], F32, tag="ps")
+                for c in range(CHUNKS):
+                    nc.tensor.matmul(
+                        out=sum_bank[:, c * P : (c + 1) * P],
+                        lhsT=gates[g][:, c, j * P : (j + 1) * P],
+                        rhs=ident_f32[:],
+                        is_transpose=True,
+                        start=(c == 0),
+                        stop=False,
+                    )
+                nc.tensor.matmul(
+                    out=sum_bank[:], lhsT=neg_ident[:], rhs=m_rows[g][:, j * HID : (j + 1) * HID],
+                    start=False, stop=True,
+                )
+                sum_banks.append(sum_bank)
+            banks[s] = (i_banks, sum_banks)
+
+        def chain(s):
+            i_banks, sum_banks = banks[s]
+            args = arg_pool.tile([P, 2, PAIR_TILES * HID], F32, tag="args")
+            i_arg = args[:, 0, :]
+            f_arg = args[:, 1, :]
+            m_t = m_t_pool.tile([P, PAIR_TILES * HID], F32, tag="m_t")
+            tile_cols = [slice(t * HID, (t + 1) * HID) for t in range(PAIR_TILES)]
+            for t, cols in enumerate(tile_cols):
+                nc.vector.tensor_tensor(out=i_arg[:, cols], in0=i_banks[t][:], in1=bi_all[:], op=ALU.add)
+            for t, cols in enumerate(tile_cols):
+                nc.vector.scalar_tensor_tensor(
+                    out=m_t[:, cols], in0=sum_banks[t][:], scalar=-1.0, in1=i_arg[:, cols], op0=ALU.mult, op1=ALU.max
+                )
+            for t, cols in enumerate(tile_cols):
+                nc.vector.scalar_tensor_tensor(
+                    out=f_arg[:, cols], in0=sum_banks[t][:], scalar=-1.0, in1=m_t[:, cols], op0=ALU.mult, op1=ALU.subtract
+                )
+            nc.gpsimd.tensor_tensor(out=i_arg, in0=i_arg, in1=m_t[:], op=ALU.subtract)
+            nc.sync.dma_start(out=pair_rows(out_0, s), in_=m_t[:])
+            pair_args[s] = args
+
+        def exponentials(s):
+            both = pair_args[s][:].rearrange("p a w -> p (a w)")
+            nc.scalar.activation(out=both, in_=both, func=ACT.Exp)
+            nc.sync.dma_start(out=pair_rows(out_1, s), in_=pair_args[s][:, 0, :])
+            nc.sync.dma_start(out=pair_rows(out_2, s), in_=pair_args[s][:, 1, :])
+
+        bias_rows = consts.tile([P, P], BF16, tag="bias_rows")
+        nc.vector.memset(bias_rows[:], 0.0)
+        nc.scalar.dma_start(out=bias_rows[0:CHUNKS, :], in_=b_f.rearrange("(c p) -> c p", p=P))
+        one = consts.tile([P, 1], F32, tag="one")
+        nc.vector.memset(one[:], 1.0)
+        warm = consts.tile([P, 1], F32, tag="warm")
+        nc.scalar.activation(out=warm[:], in_=one[:], func=ACT.Exp)
+        neg_ident = consts.tile([P, P], BF16, tag="neg_ident")
+        nc.vector.tensor_scalar(out=neg_ident[:], in0=ident_bf16[:], scalar1=-1.0, scalar2=None, op0=ALU.mult)
+        wfx_raw = load_weight(Wf_x)
+        wfh_raw = load_weight(Wf_h)
+        load_group_activations(0)
+
+        bias_bank = psum.tile([P, P], BF16, tag="tr")
+        nc.tensor.transpose(bias_bank[:], bias_rows[:], ident_bf16[:])
+        neg_bf = consts.tile([P, CHUNKS], F32, tag="neg_bf")
+        nc.vector.tensor_scalar(
+            out=neg_bf[:], in0=bias_bank[:, 0:CHUNKS], scalar1=-1.0, scalar2=None, op0=ALU.mult
+        )
+
+        weights["fx"] = prepare_weight(wfx_raw, "wfx", "x", nc.scalar.copy)
+        weights["fh"] = prepare_weight(wfh_raw, "wfh", "h", nc.scalar.copy)
+
+        wix_raw = load_weight(Wi_x)
+        load_group_activations(1)
+        wih_raw = load_weight(Wi_h)
+        bi_all = consts.tile([P, HID], BF16, tag="bi_all")
+        nc.sync.dma_start(out=bi_all[:], in_=b_i.partition_broadcast(P))
+        load_activations(1)
+        load_m_prev(0)
+
+        prepare_group(0, nc.scalar.copy)
+        start_group(1, "ps")
+        weights["ix"] = prepare_weight(wix_raw, "wix", "x", nc.vector.tensor_copy)
+        forget_gate(0)
+        middle_group(1, nc.vector.tensor_copy)
+        finish_group(1, nc.vector.tensor_copy)
+        start_group(2, "ps")
+        weights["ih"] = prepare_weight(wih_raw, "wih", "h", nc.vector.tensor_copy)
+        forget_gate(1)
+        logarithms(0)
+        load_activations(2)
+        middle_group(2, nc.vector.tensor_copy)
+        finish_group(2, nc.vector.tensor_copy)
+        prepare_group(3, nc.vector.tensor_copy)
+        load_activations(3)
+        chain_banks(0)
+
+        for k in range(N_ROUNDS):
+            load_m_prev(k + 1)
+            for g in round_groups(k + 1):
+                forget_gate(g)
+            logarithms(k + 1)
+            round_pairs = range(k * ROUND_PAIRS, (k + 1) * ROUND_PAIRS)
+            coming = round_groups(k + 2)
+            last_round = k == N_ROUNDS - 1
+            for s in round_pairs:
+                chain(s)
+                if s == round_pairs[-1] and coming:
+                    start_group(coming[0], "tr")
+                if s + 1 < N_PAIRS:
+                    chain_banks(s + 1)
+                if last_round:
+                    exponentials(s)
+            for g in coming:
+                if g != coming[0]:
+                    start_group(g, "tr")
+                middle_group(g, nc.vector.tensor_copy)
+                finish_group(g, nc.vector.tensor_copy)
+            if not last_round:
+                for s in round_pairs:
+                    exponentials(s)

@@ -23,12 +23,8 @@ PAIR_ROWS = PAIR_TILES * P
 GROUP_PAIRS = 2
 GROUP_TILES = GROUP_PAIRS * PAIR_TILES
 GROUP_ROWS = GROUP_TILES * P
-ROUND_GROUPS = 2
-ROUND_PAIRS = ROUND_GROUPS * GROUP_PAIRS
 N_GROUPS = BATCH // GROUP_ROWS
-N_ROUNDS = N_GROUPS // ROUND_GROUPS
 N_PAIRS = BATCH // PAIR_ROWS
-assert ROUND_GROUPS == 2
 
 E_MAX = 1.0e8 - 1.0
 
@@ -41,12 +37,11 @@ def tile_slstmlayer_pa_t_kernel(
     nc = tc.nc
     with ExitStack() as ctx:
         consts = ctx.enter_context(tc.tile_pool(name="consts", bufs=1))
-        raws = ctx.enter_context(tc.tile_pool(name="raws", bufs=4 * ROUND_GROUPS))
-        m_pool = ctx.enter_context(tc.tile_pool(name="m_pool", bufs=2 * ROUND_GROUPS))
+        raws = ctx.enter_context(tc.tile_pool(name="raws", bufs=7))
         grouped_pool = ctx.enter_context(tc.tile_pool(name="grouped_pool", bufs=2))
-        codes_pool = ctx.enter_context(tc.tile_pool(name="codes_pool", bufs=3 * ROUND_GROUPS))
-        gate_pool = ctx.enter_context(tc.tile_pool(name="gate_pool", bufs=2 * ROUND_GROUPS))
-        arg_pool = ctx.enter_context(tc.tile_pool(name="arg_pool", bufs=ROUND_PAIRS + 3))
+        codes_pool = ctx.enter_context(tc.tile_pool(name="codes_pool", bufs=4))
+        gate_pool = ctx.enter_context(tc.tile_pool(name="gate_pool", bufs=3))
+        arg_pool = ctx.enter_context(tc.tile_pool(name="arg_pool", bufs=4))
         m_t_pool = ctx.enter_context(tc.tile_pool(name="m_t_pool", bufs=4))
         psum = ctx.enter_context(tc.psum_pool(name="psum", bufs=2))
         ctx.enter_context(tc.manual_schedule())
@@ -56,199 +51,190 @@ def tile_slstmlayer_pa_t_kernel(
         ident_bf16 = consts.tile([P, P], BF16, tag="ident_bf16")
         make_identity(nc, ident_bf16[:])
 
-        def pair_rows(dram, s):
-            rows = dram[s * PAIR_ROWS : (s + 1) * PAIR_ROWS, :]
-            return rows.rearrange("(p t) k -> p (t k)", t=PAIR_TILES)
-
-        def load_group(rows_tile, dram, g):
+        def group_view(dram, g):
             rows = dram[g * GROUP_ROWS : (g + 1) * GROUP_ROWS, :]
+            return rows.rearrange("(p t) k -> p t k", t=GROUP_TILES)
+
+        def pair_view(dram, s):
+            g, half = divmod(s, GROUP_PAIRS)
+            return group_view(dram, g)[:, half * PAIR_TILES : (half + 1) * PAIR_TILES, :]
+
+        raw = {}
+
+        def new_raw(name, g):
+            raw[name, g] = raws.tile([P, GROUP_TILES, FEAT], BF16, tag=name, name=name)
+
+        def load_group(name, dram, g):
+            new_raw(name, g)
+            nc.sync.dma_start(out=raw[name, g][:], in_=group_view(dram, g))
+
+        def load_pair(name, dram, s):
+            g, half = divmod(s, GROUP_PAIRS)
             nc.sync.dma_start(
-                out=rows_tile[:].rearrange("p (a w) -> p a w", a=GROUP_PAIRS),
-                in_=rows.rearrange("(a p t) k -> p a (t k)", a=GROUP_PAIRS, t=PAIR_TILES),
+                out=raw[name, g][:, half * PAIR_TILES : (half + 1) * PAIR_TILES, :], in_=pair_view(dram, s)
             )
 
-        def load_weight(w):
-            raw = raws.tile([P, GROUP_TILES * FEAT], BF16, tag="w_raw", bufs=2)
-            nc.sync.dma_start(
-                out=raw[:].rearrange("p (c k) -> p c k", c=CHUNKS),
-                in_=w.rearrange("(c p) k -> p c k", p=P),
-            )
-            return raw
+        def load_weight(w, name):
+            tile = consts.tile([P, CHUNKS, FEAT], BF16, tag=name, name=name)
+            nc.sync.dma_start(out=tile[:], in_=w.rearrange("(c p) k -> p c k", p=P))
+            return tile
 
-        x_raw = {}
-        h_raw = {}
-        m_rows = {}
-
-        def round_groups(k):
-            return range(k * ROUND_GROUPS, (k + 1) * ROUND_GROUPS) if k < N_ROUNDS else ()
-
-        def load_group_activations(g):
-            x_raw[g] = raws.tile([P, GROUP_TILES * FEAT], BF16, tag="raw", name="x_raw")
-            load_group(x_raw[g], x, g)
-            h_raw[g] = raws.tile([P, GROUP_TILES * FEAT], BF16, tag="raw", name="h_raw")
-            load_group(h_raw[g], h_prev, g)
-
-        def load_activations(k):
-            for g in round_groups(k):
-                load_group_activations(g)
-
-        def load_m_prev(k):
-            for g in round_groups(k):
-                m_rows[g] = m_pool.tile([P, GROUP_TILES * HID], BF16, tag="m", name="m_rows")
-                load_group(m_rows[g], m_prev, g)
-
-        def new_operand(raw, pool, name, side):
-            grouped = grouped_pool.tile([P, 4 * GROUP_ROWS], BF16, tag=side + "_grouped", align_bytes=64)
-            codes = pool.tile([P, GROUP_ROWS], U32, tag=name + "_codes", align_bytes=64)
-            scales = pool.tile([P, GROUP_ROWS], U8, tag=name + "_scales", align_bytes=64)
-            return {"raw": raw, "grouped": grouped, "codes": codes, "scales": scales}
-
-        def transpose_half(operand, half, bank_tag):
-            words = operand["raw"][:].bitcast(F32)
-            bank = psum.tile([P, 2, PAIR_ROWS], F32, tag=bank_tag)
+        def transpose_rows(rows, first_tile, tag):
+            words = rows[:].rearrange("p t k -> p (t k)").bitcast(F32)
+            bank = psum.tile([P, 2, PAIR_ROWS], F32, tag=tag, name="word_bank")
             for t in range(PAIR_TILES):
+                row = (first_tile + t) * WORDS
                 for u in range(2):
-                    row = (half * PAIR_TILES + t) * WORDS
                     nc.tensor.transpose(
                         bank[:, u, t * P : (t + 1) * P], words[:, row + u : row + WORDS : 2], ident_f32[:]
                     )
             return bank
 
-        def copy_out_half(operand, half, bank, copy):
-            words = operand["grouped"][:].bitcast(F32)[:, half * 2 * PAIR_ROWS : (half + 1) * 2 * PAIR_ROWS]
+        def copy_out(grouped, part, bank, copy):
+            words = grouped[:].bitcast(F32)[:, part * 2 * PAIR_ROWS : (part + 1) * 2 * PAIR_ROWS]
             copy(out=words.rearrange("p (r u) -> p r u", u=2), in_=bank[:].rearrange("p u r -> p r u"))
 
-        def quantise(operand):
+        def new_operand(pool, name):
+            grouped = grouped_pool.tile([P, 8 * PAIR_ROWS], BF16, tag=name + "_grouped", name="grouped", align_bytes=64)
+            codes = pool.tile([P, 2 * PAIR_ROWS], U32, tag=name + "_codes", name="codes", align_bytes=64)
+            scales = pool.tile([P, 2 * PAIR_ROWS], U8, tag=name + "_scales", name="scales", align_bytes=64)
+            return {"grouped": grouped, "codes": codes, "scales": scales}
+
+        def quantise(op):
             nc.vector.quantize_mx(
-                out=operand["codes"][:].bitcast(FP8X4), scales=operand["scales"][:], in_=operand["grouped"][:]
+                out=op["codes"][:].bitcast(FP8X4), scales=op["scales"][:], in_=op["grouped"][:]
             )
 
-        def prepare_weight(raw, name, side, second_copy):
-            operand = new_operand(raw, consts, name, side)
-            copy_out_half(operand, 0, transpose_half(operand, 0, "pi"), nc.vector.tensor_copy)
-            copy_out_half(operand, 1, transpose_half(operand, 1, "pi"), second_copy)
-            quantise(operand)
-            return operand
-
-        def mx_product(out, stationary, stationary_cols, moving, start, stop):
+        def mx(out, lhs, lhs_cols, rhs, rhs_cols, start, stop):
             nc.tensor.matmul_mx(
                 out=out,
-                lhsT=stationary["codes"][:, stationary_cols].bitcast(FP8X4),
-                lhsT_scale=stationary["scales"][:, stationary_cols],
-                rhs=moving["codes"][:].bitcast(FP8X4),
-                rhs_scale=moving["scales"][:],
+                lhsT=lhs["codes"][:, lhs_cols].bitcast(FP8X4),
+                lhsT_scale=lhs["scales"][:, lhs_cols],
+                rhs=rhs["codes"][:, rhs_cols].bitcast(FP8X4),
+                rhs_scale=rhs["scales"][:, rhs_cols],
                 start=start,
                 stop=stop,
             )
 
         weights = {}
-        x_ops = {}
-        h_ops = {}
+        wbanks = {}
+        ops = {}
+        tr_banks = {}
         gates = {}
-        word_banks = {}
-        banks = {}
-        pair_args = {}
+        f_banks = {}
+        i_banks = {}
+        s_banks = {}
+        args = {}
+        X_COLS = slice(0, PAIR_ROWS)
+        H_COLS = slice(PAIR_ROWS, 2 * PAIR_ROWS)
 
-        def forget_gate(g):
-            gates[g] = gate_pool.tile([P, CHUNKS, GROUP_ROWS], F32, tag="gate", name="gate")
+        def weight_T(rows, name, tags):
+            wbanks[name] = [transpose_rows(rows, 0, tags), transpose_rows(rows, PAIR_TILES, tags)]
+
+        def weight_copy(name, copies):
+            weights[name] = new_operand(consts, name)
+            for part in range(2):
+                copy_out(weights[name]["grouped"], part, wbanks[name][part], copies[part])
+
+        def prep_T(s, tag="tr"):
+            g, half = divmod(s, GROUP_PAIRS)
+            tr_banks[s] = [transpose_rows(raw[n, g], half * PAIR_TILES, tag) for n in ("x", "h")]
+
+        def prep_copy(s, copies):
+            ops[s] = new_operand(codes_pool, "act")
+            for part in range(2):
+                copy_out(ops[s]["grouped"], part, tr_banks[s][part], copies[part])
+
+        def f_T(s):
+            f_banks[s] = []
+            for b in range(2):
+                bank = psum.tile([P, 2, PAIR_ROWS], F32, tag="pf", name="f_bank")
+                for j in range(2):
+                    cols = slice((2 * b + j) * P, (2 * b + j + 1) * P)
+                    mx(bank[:, j, :], weights["fx"], cols, ops[s], X_COLS, True, False)
+                    mx(bank[:, j, :], weights["fh"], cols, ops[s], H_COLS, False, True)
+                f_banks[s].append(bank)
+
+        def f_exp(s):
+            gates[s] = gate_pool.tile([P, CHUNKS, PAIR_ROWS], F32, tag="gate", name="gate")
             for c in range(CHUNKS):
-                f_bank = psum.tile([P, GROUP_ROWS], F32, tag="pf")
-                chunk_cols = slice(c * P, (c + 1) * P)
-                mx_product(f_bank[:], weights["fx"], chunk_cols, x_ops[g], True, False)
-                mx_product(f_bank[:], weights["fh"], chunk_cols, h_ops[g], False, True)
                 nc.scalar.activation(
-                    out=gates[g][:, c, :], in_=f_bank[:], func=ACT.Exp,
+                    out=gates[s][:, c, :], in_=f_banks[s][c // 2][:, c % 2, :], func=ACT.Exp,
                     bias=neg_bf[:, c : c + 1], scale=-1.0,
                 )
-                nc.gpsimd.tensor_scalar(
-                    out=gates[g][:, c, :], in0=gates[g][:, c, :],
-                    scalar1=E_MAX, scalar2=0.0, op0=ALU.min, op1=ALU.max,
-                )
 
-        def logarithms(k):
-            for g in round_groups(k):
-                flat = gates[g][:].rearrange("p c b -> p (c b)")
-                nc.scalar.activation(out=flat, in_=flat, func=ACT.Ln, bias=one[:], scale=1.0)
+        def f_clamp(s):
+            flat = gates[s][:].rearrange("p c b -> p (c b)")
+            nc.gpsimd.tensor_scalar(out=flat, in0=flat, scalar1=E_MAX, scalar2=0.0, op0=ALU.min, op1=ALU.max)
 
-        def start_group(g, bank_tag):
-            x_ops[g] = new_operand(x_raw[g], codes_pool, "x", "x")
-            h_ops[g] = new_operand(h_raw[g], codes_pool, "h", "h")
-            word_banks[g] = (transpose_half(x_ops[g], 0, bank_tag), transpose_half(h_ops[g], 0, bank_tag))
+        def f_log(s):
+            flat = gates[s][:].rearrange("p c b -> p (c b)")
+            nc.scalar.activation(out=flat, in_=flat, func=ACT.Ln, bias=one[:], scale=1.0)
 
-        def middle_group(g, h_copy):
-            x_bank, h_bank = word_banks[g]
-            copy_out_half(x_ops[g], 0, x_bank, nc.vector.tensor_copy)
-            copy_out_half(h_ops[g], 0, h_bank, h_copy)
-            word_banks[g] = (transpose_half(x_ops[g], 1, "tr"), transpose_half(h_ops[g], 1, "tr"))
+        def i_T(s):
+            i_banks[s] = []
+            for t in range(PAIR_TILES):
+                bank = psum.tile([P, HID], F32, tag="pi", name="i_bank")
+                mx(bank[:], ops[s], slice(t * P, (t + 1) * P), weights["ix"], slice(0, HID), True, False)
+                mx(bank[:], ops[s], slice(PAIR_ROWS + t * P, PAIR_ROWS + (t + 1) * P), weights["ih"], slice(0, HID), False, True)
+                i_banks[s].append(bank)
 
-        def finish_group(g, h_copy):
-            x_bank, h_bank = word_banks[g]
-            copy_out_half(x_ops[g], 1, x_bank, nc.vector.tensor_copy)
-            copy_out_half(h_ops[g], 1, h_bank, h_copy)
-            quantise(x_ops[g])
-            quantise(h_ops[g])
-
-        def prepare_group(g, h_copy):
-            start_group(g, "tr")
-            middle_group(g, h_copy)
-            finish_group(g, h_copy)
-
-        def chain_banks(s):
+        def s_T(s):
             g, half = divmod(s, GROUP_PAIRS)
-            i_banks = []
+            s_banks[s] = []
             for t in range(PAIR_TILES):
-                j = half * PAIR_TILES + t
-                i_bank = psum.tile([P, HID], F32, tag="pi")
-                tile_cols = slice(j * P, (j + 1) * P)
-                mx_product(i_bank[:], x_ops[g], tile_cols, weights["ix"], True, False)
-                mx_product(i_bank[:], h_ops[g], tile_cols, weights["ih"], False, True)
-                i_banks.append(i_bank)
-            sum_banks = []
-            for t in range(PAIR_TILES):
-                j = half * PAIR_TILES + t
-                sum_bank = psum.tile([P, HID], F32, tag="ps")
+                bank = psum.tile([P, HID], F32, tag="ps", name="s_bank")
                 for c in range(CHUNKS):
                     nc.tensor.matmul(
-                        out=sum_bank[:, c * P : (c + 1) * P],
-                        lhsT=gates[g][:, c, j * P : (j + 1) * P],
+                        out=bank[:, c * P : (c + 1) * P],
+                        lhsT=gates[s][:, c, t * P : (t + 1) * P],
                         rhs=ident_f32[:],
                         is_transpose=True,
                         start=(c == 0),
                         stop=False,
                     )
                 nc.tensor.matmul(
-                    out=sum_bank[:], lhsT=neg_ident[:], rhs=m_rows[g][:, j * HID : (j + 1) * HID],
-                    start=False, stop=True,
+                    out=bank[:], lhsT=neg_ident[:], rhs=raw["m", g][:, half * PAIR_TILES + t, :], start=False, stop=True
                 )
-                sum_banks.append(sum_bank)
-            banks[s] = (i_banks, sum_banks)
+                s_banks[s].append(bank)
 
-        def chain(s):
-            i_banks, sum_banks = banks[s]
-            args = arg_pool.tile([P, 2, PAIR_TILES * HID], F32, tag="args")
-            i_arg = args[:, 0, :]
-            f_arg = args[:, 1, :]
-            m_t = m_t_pool.tile([P, PAIR_TILES * HID], F32, tag="m_t")
-            tile_cols = [slice(t * HID, (t + 1) * HID) for t in range(PAIR_TILES)]
-            for t, cols in enumerate(tile_cols):
-                nc.vector.tensor_tensor(out=i_arg[:, cols], in0=i_banks[t][:], in1=bi_all[:], op=ALU.add)
-            for t, cols in enumerate(tile_cols):
+        m_ts = {}
+
+        def chain_i(s):
+            args[s] = arg_pool.tile([P, 2, PAIR_TILES * HID], F32, tag="args", name="args")
+            m_ts[s] = m_t_pool.tile([P, PAIR_TILES * HID], F32, tag="m_t", name="m_t")
+            for t in range(PAIR_TILES):
+                cols = slice(t * HID, (t + 1) * HID)
+                nc.vector.tensor_tensor(out=args[s][:, 0, cols], in0=i_banks[s][t][:], in1=bi_all[:], op=ALU.add)
+
+        def chain_m(s):
+            for t in range(PAIR_TILES):
+                cols = slice(t * HID, (t + 1) * HID)
                 nc.vector.scalar_tensor_tensor(
-                    out=m_t[:, cols], in0=sum_banks[t][:], scalar=-1.0, in1=i_arg[:, cols], op0=ALU.mult, op1=ALU.max
+                    out=m_ts[s][:, cols], in0=s_banks[s][t][:], scalar=-1.0, in1=args[s][:, 0, cols], op0=ALU.mult, op1=ALU.max
                 )
-            for t, cols in enumerate(tile_cols):
+            nc.sync.dma_start(out=pair_view(out_0, s), in_=m_ts[s][:].rearrange("p (t k) -> p t k", t=PAIR_TILES))
+
+        def chain_g(s):
+            for t in range(PAIR_TILES):
+                cols = slice(t * HID, (t + 1) * HID)
+                nc.gpsimd.tensor_tensor(out=args[s][:, 0, cols], in0=args[s][:, 0, cols], in1=m_ts[s][:, cols], op=ALU.subtract)
+
+        def chain_f(s):
+            for t in range(PAIR_TILES):
+                cols = slice(t * HID, (t + 1) * HID)
                 nc.vector.scalar_tensor_tensor(
-                    out=f_arg[:, cols], in0=sum_banks[t][:], scalar=-1.0, in1=m_t[:, cols], op0=ALU.mult, op1=ALU.subtract
+                    out=args[s][:, 1, cols], in0=s_banks[s][t][:], scalar=-1.0, in1=m_ts[s][:, cols], op0=ALU.mult, op1=ALU.subtract
                 )
-            nc.gpsimd.tensor_tensor(out=i_arg, in0=i_arg, in1=m_t[:], op=ALU.subtract)
-            nc.sync.dma_start(out=pair_rows(out_0, s), in_=m_t[:])
-            pair_args[s] = args
 
         def exponentials(s):
-            both = pair_args[s][:].rearrange("p a w -> p (a w)")
+            both = args[s][:].rearrange("p a w -> p (a w)")
             nc.scalar.activation(out=both, in_=both, func=ACT.Exp)
-            nc.sync.dma_start(out=pair_rows(out_1, s), in_=pair_args[s][:, 0, :])
-            nc.sync.dma_start(out=pair_rows(out_2, s), in_=pair_args[s][:, 1, :])
+            nc.sync.dma_start(out=pair_view(out_1, s), in_=args[s][:, 0, :].rearrange("p (t k) -> p t k", t=PAIR_TILES))
+            nc.sync.dma_start(out=pair_view(out_2, s), in_=args[s][:, 1, :].rearrange("p (t k) -> p t k", t=PAIR_TILES))
+
+        V = nc.vector.tensor_copy
+        A = nc.scalar.copy
 
         bias_rows = consts.tile([P, P], BF16, tag="bias_rows")
         nc.vector.memset(bias_rows[:], 0.0)
@@ -259,66 +245,87 @@ def tile_slstmlayer_pa_t_kernel(
         nc.scalar.activation(out=warm[:], in_=one[:], func=ACT.Exp)
         neg_ident = consts.tile([P, P], BF16, tag="neg_ident")
         nc.vector.tensor_scalar(out=neg_ident[:], in0=ident_bf16[:], scalar1=-1.0, scalar2=None, op0=ALU.mult)
-        wfx_raw = load_weight(Wf_x)
-        wfh_raw = load_weight(Wf_h)
-        load_group_activations(0)
 
-        bias_bank = psum.tile([P, P], BF16, tag="tr")
-        nc.tensor.transpose(bias_bank[:], bias_rows[:], ident_bf16[:])
-        neg_bf = consts.tile([P, CHUNKS], F32, tag="neg_bf")
-        nc.vector.tensor_scalar(
-            out=neg_bf[:], in0=bias_bank[:, 0:CHUNKS], scalar1=-1.0, scalar2=None, op0=ALU.mult
-        )
-
-        weights["fx"] = prepare_weight(wfx_raw, "wfx", "x", nc.scalar.copy)
-        weights["fh"] = prepare_weight(wfh_raw, "wfh", "h", nc.scalar.copy)
-
-        wix_raw = load_weight(Wi_x)
-        load_group_activations(1)
-        wih_raw = load_weight(Wi_h)
+        new_raw("x", 0)
+        new_raw("h", 0)
+        load_pair("x", x, 0)
+        wfx_raw = load_weight(Wf_x, "wfx_raw")
+        load_pair("h", h_prev, 0)
+        wfh_raw = load_weight(Wf_h, "wfh_raw")
+        load_pair("x", x, 1)
+        load_pair("h", h_prev, 1)
+        wix_raw = load_weight(Wi_x, "wix_raw")
+        wih_raw = load_weight(Wi_h, "wih_raw")
+        load_group("x", x, 1)
+        load_group("h", h_prev, 1)
         bi_all = consts.tile([P, HID], BF16, tag="bi_all")
         nc.sync.dma_start(out=bi_all[:], in_=b_i.partition_broadcast(P))
-        load_activations(1)
-        load_m_prev(0)
+        load_group("m", m_prev, 0)
+        for g in range(2, N_GROUPS):
+            load_group("x", x, g)
+            load_group("h", h_prev, g)
+            load_group("m", m_prev, g - 1)
+        load_group("m", m_prev, N_GROUPS - 1)
 
-        prepare_group(0, nc.scalar.copy)
-        start_group(1, "ps")
-        weights["ix"] = prepare_weight(wix_raw, "wix", "x", nc.vector.tensor_copy)
-        forget_gate(0)
-        middle_group(1, nc.vector.tensor_copy)
-        finish_group(1, nc.vector.tensor_copy)
-        start_group(2, "ps")
-        weights["ih"] = prepare_weight(wih_raw, "wih", "h", nc.vector.tensor_copy)
-        forget_gate(1)
-        logarithms(0)
-        load_activations(2)
-        middle_group(2, nc.vector.tensor_copy)
-        finish_group(2, nc.vector.tensor_copy)
-        prepare_group(3, nc.vector.tensor_copy)
-        load_activations(3)
-        chain_banks(0)
+        bias_bank = psum.tile([P, P], BF16, tag="tr", name="bias_bank")
+        nc.tensor.transpose(bias_bank[:], bias_rows[:], ident_bf16[:])
+        neg_bf = consts.tile([P, CHUNKS], F32, tag="neg_bf")
+        nc.vector.tensor_scalar(out=neg_bf[:], in0=bias_bank[:, 0:CHUNKS], scalar1=-1.0, scalar2=None, op0=ALU.mult)
 
-        for k in range(N_ROUNDS):
-            load_m_prev(k + 1)
-            for g in round_groups(k + 1):
-                forget_gate(g)
-            logarithms(k + 1)
-            round_pairs = range(k * ROUND_PAIRS, (k + 1) * ROUND_PAIRS)
-            coming = round_groups(k + 2)
-            last_round = k == N_ROUNDS - 1
-            for s in round_pairs:
-                chain(s)
-                if s == round_pairs[-1] and coming:
-                    start_group(coming[0], "tr")
-                if s + 1 < N_PAIRS:
-                    chain_banks(s + 1)
-                if last_round:
-                    exponentials(s)
-            for g in coming:
-                if g != coming[0]:
-                    start_group(g, "tr")
-                middle_group(g, nc.vector.tensor_copy)
-                finish_group(g, nc.vector.tensor_copy)
-            if not last_round:
-                for s in round_pairs:
-                    exponentials(s)
+        weight_T(wfx_raw, "fx", "pi")
+        prep_T(0)
+        weight_T(wfh_raw, "fh", "ps")
+        weight_copy("fx", (V, A))
+        prep_copy(0, (V, A))
+        quantise(weights["fx"])
+        weight_copy("fh", (V, A))
+        quantise(ops[0])
+        quantise(weights["fh"])
+        prep_T(1)
+        f_T(0)
+        f_exp(0)
+        f_clamp(0)
+        prep_copy(1, (V, V))
+        weight_T(wix_raw, "ix", "pi")
+        weight_T(wih_raw, "ih", "ps")
+        quantise(ops[1])
+        f_log(0)
+        weight_copy("ix", (V, A))
+        weight_copy("ih", (V, A))
+        quantise(weights["ix"])
+        f_T(1)
+        f_exp(1)
+        f_clamp(1)
+        prep_T(2)
+        quantise(weights["ih"])
+        i_T(0)
+        s_T(0)
+        prep_copy(2, (V, V))
+        f_log(1)
+        quantise(ops[2])
+
+        for k in range(N_PAIRS):
+            chain_i(k)
+            if k + 3 < N_PAIRS:
+                prep_T(k + 3)
+            chain_m(k)
+            chain_g(k)
+            if k + 3 < N_PAIRS:
+                prep_copy(k + 3, (V, A if k % 2 else V))
+            chain_f(k)
+            if k + 1 < N_PAIRS:
+                i_T(k + 1)
+            if k + 2 < N_PAIRS:
+                f_T(k + 2)
+                f_exp(k + 2)
+            if k + 3 < N_PAIRS:
+                quantise(ops[k + 3])
+            if k + 2 < N_PAIRS:
+                f_clamp(k + 2)
+            if k > 0:
+                exponentials(k - 1)
+            if k + 1 < N_PAIRS:
+                s_T(k + 1)
+            if k + 2 < N_PAIRS:
+                f_log(k + 2)
+        exponentials(N_PAIRS - 1)

@@ -28,6 +28,9 @@ N_PAIRS = BATCH // PAIR_ROWS
 
 E_MAX = 1.0e8 - 1.0
 
+ROUND = 4
+LOAD_AHEAD = 5
+
 FLOPS = 2 * BATCH * HID * FEAT * 4
 
 
@@ -37,12 +40,12 @@ def tile_slstmlayer_pa_t_kernel(
     nc = tc.nc
     with ExitStack() as ctx:
         consts = ctx.enter_context(tc.tile_pool(name="consts", bufs=1))
-        raws = ctx.enter_context(tc.tile_pool(name="raws", bufs=7))
+        raws = ctx.enter_context(tc.tile_pool(name="raws", bufs=5))
         grouped_pool = ctx.enter_context(tc.tile_pool(name="grouped_pool", bufs=2))
-        codes_pool = ctx.enter_context(tc.tile_pool(name="codes_pool", bufs=4))
-        gate_pool = ctx.enter_context(tc.tile_pool(name="gate_pool", bufs=3))
-        arg_pool = ctx.enter_context(tc.tile_pool(name="arg_pool", bufs=4))
-        m_t_pool = ctx.enter_context(tc.tile_pool(name="m_t_pool", bufs=4))
+        codes_pool = ctx.enter_context(tc.tile_pool(name="codes_pool", bufs=7))
+        gate_pool = ctx.enter_context(tc.tile_pool(name="gate_pool", bufs=6))
+        arg_pool = ctx.enter_context(tc.tile_pool(name="arg_pool", bufs=6))
+        m_t_pool = ctx.enter_context(tc.tile_pool(name="m_t_pool", bufs=3))
         psum = ctx.enter_context(tc.psum_pool(name="psum", bufs=2))
         ctx.enter_context(tc.manual_schedule())
 
@@ -131,19 +134,22 @@ def tile_slstmlayer_pa_t_kernel(
         def weight_T(rows, name, tags):
             wbanks[name] = [transpose_rows(rows, 0, tags), transpose_rows(rows, PAIR_TILES, tags)]
 
-        def weight_copy(name, copies):
-            weights[name] = new_operand(consts, name)
-            for part in range(2):
+        def weight_copy(name, copies, parts=(0, 1)):
+            if name not in weights:
+                weights[name] = new_operand(consts, name)
+            for part in parts:
                 copy_out(weights[name]["grouped"], part, wbanks[name][part], copies[part])
 
-        def prep_T(s, tag="tr"):
+        def prep_T(s, parts=(0, 1)):
             g, half = divmod(s, GROUP_PAIRS)
-            tr_banks[s] = [transpose_rows(raw[n, g], half * PAIR_TILES, tag) for n in ("x", "h")]
+            for part in parts:
+                tr_banks[s, part] = transpose_rows(raw["xh"[part], g], half * PAIR_TILES, "tr")
 
-        def prep_copy(s, copies):
-            ops[s] = new_operand(codes_pool, "act")
-            for part in range(2):
-                copy_out(ops[s]["grouped"], part, tr_banks[s][part], copies[part])
+        def prep_copy(s, copies, parts=(0, 1)):
+            if s not in ops:
+                ops[s] = new_operand(codes_pool, "act")
+            for part in parts:
+                copy_out(ops[s]["grouped"], part, tr_banks[s, part], copies[part])
 
         def f_T(s):
             f_banks[s] = []
@@ -164,8 +170,9 @@ def tile_slstmlayer_pa_t_kernel(
                 )
 
         def f_clamp(s):
-            flat = gates[s][:].rearrange("p c b -> p (c b)")
-            nc.gpsimd.tensor_scalar(out=flat, in0=flat, scalar1=E_MAX, scalar2=0.0, op0=ALU.min, op1=ALU.max)
+            for b in range(2):
+                flat = gates[s][:, 2 * b : 2 * b + 2, :].rearrange("p c b -> p (c b)")
+                nc.gpsimd.tensor_scalar(out=flat, in0=flat, scalar1=E_MAX, scalar2=0.0, op0=ALU.min, op1=ALU.max)
 
         def f_log(s):
             flat = gates[s][:].rearrange("p c b -> p (c b)")
@@ -261,71 +268,87 @@ def tile_slstmlayer_pa_t_kernel(
         bi_all = consts.tile([P, HID], BF16, tag="bi_all")
         nc.sync.dma_start(out=bi_all[:], in_=b_i.partition_broadcast(P))
         load_group("m", m_prev, 0)
-        for g in range(2, N_GROUPS):
+        for g in range(2, LOAD_AHEAD):
             load_group("x", x, g)
             load_group("h", h_prev, g)
             load_group("m", m_prev, g - 1)
-        load_group("m", m_prev, N_GROUPS - 1)
 
-        bias_bank = psum.tile([P, P], BF16, tag="tr", name="bias_bank")
+        prep_T(0, (0,))
+        weight_T(wfx_raw, "fx", "pi")
+        prep_T(0, (1,))
+        weight_T(wfh_raw, "fh", "ps")
+        prep_copy(0, (V, A), (0,))
+        weight_copy("fx", (A, V))
+        prep_copy(0, (V, A), (1,))
+        weight_copy("fh", (V, A))
+        quantise(weights["fx"])
+        quantise(ops[0])
+        bias_bank = psum.tile([P, P], BF16, tag="pf", name="bias_bank")
         nc.tensor.transpose(bias_bank[:], bias_rows[:], ident_bf16[:])
         neg_bf = consts.tile([P, CHUNKS], F32, tag="neg_bf")
         nc.vector.tensor_scalar(out=neg_bf[:], in0=bias_bank[:, 0:CHUNKS], scalar1=-1.0, scalar2=None, op0=ALU.mult)
-
-        weight_T(wfx_raw, "fx", "pi")
-        prep_T(0)
-        weight_T(wfh_raw, "fh", "ps")
-        weight_copy("fx", (V, A))
-        prep_copy(0, (V, A))
-        quantise(weights["fx"])
-        weight_copy("fh", (V, A))
-        quantise(ops[0])
         quantise(weights["fh"])
+
+        def forget(s):
+            f_T(s)
+            f_exp(s)
+            f_clamp(s)
+
         prep_T(1)
-        f_T(0)
-        f_exp(0)
-        f_clamp(0)
-        prep_copy(1, (V, V))
-        weight_T(wix_raw, "ix", "pi")
-        weight_T(wih_raw, "ih", "ps")
-        quantise(ops[1])
-        f_log(0)
-        weight_copy("ix", (V, A))
-        weight_copy("ih", (V, A))
-        quantise(weights["ix"])
-        f_T(1)
-        f_exp(1)
-        f_clamp(1)
-        prep_T(2)
-        quantise(weights["ih"])
+        for s in range(ROUND):
+            prep_copy(s + 1, (V, A))
+            if s == 1:
+                weight_copy("ix", (V, V))
+            if s == 2:
+                weight_copy("ih", (V, V))
+            forget(s)
+            prep_T(s + 2)
+            quantise(ops[s + 1])
+            if s == 0:
+                weight_T(wix_raw, "ix", "pi")
+            if s == 1:
+                weight_T(wih_raw, "ih", "ps")
+                quantise(weights["ix"])
+            if s == 2:
+                quantise(weights["ih"])
         i_T(0)
+        for s in range(ROUND):
+            f_log(s)
         s_T(0)
-        prep_copy(2, (V, V))
-        f_log(1)
-        quantise(ops[2])
 
         for k in range(N_PAIRS):
+            g = k // GROUP_PAIRS + LOAD_AHEAD
+            if k % GROUP_PAIRS == 0 and g <= N_GROUPS:
+                load_group("m", m_prev, g - 1)
+                if g < N_GROUPS:
+                    load_group("x", x, g)
+                    load_group("h", h_prev, g)
+            e = k + ROUND
             chain_i(k)
-            if k + 3 < N_PAIRS:
-                prep_T(k + 3)
+            if e < N_PAIRS:
+                f_T(e)
+                f_exp(e)
+                f_clamp(e)
             chain_m(k)
             chain_g(k)
-            if k + 3 < N_PAIRS:
-                prep_copy(k + 3, (V, A if k % 2 else V))
-            chain_f(k)
             if k + 1 < N_PAIRS:
                 i_T(k + 1)
-            if k + 2 < N_PAIRS:
-                f_T(k + 2)
-                f_exp(k + 2)
-            if k + 3 < N_PAIRS:
-                quantise(ops[k + 3])
-            if k + 2 < N_PAIRS:
-                f_clamp(k + 2)
-            if k > 0:
+            chain_f(k)
+            first, last = k % ROUND == 0, k % ROUND == ROUND - 1 and e < N_PAIRS
+            if first and k > 0:
+                exponentials(k - 2)
+            if k > 0 and not last:
                 exponentials(k - 1)
+            p = e + 1
+            if p < N_PAIRS:
+                prep_copy(p, (V, V))
+            if last:
+                for s in range(k + 1, k + 1 + ROUND):
+                    f_log(s)
             if k + 1 < N_PAIRS:
                 s_T(k + 1)
-            if k + 2 < N_PAIRS:
-                f_log(k + 2)
+            if p + 1 < N_PAIRS:
+                prep_T(p + 1)
+            if p < N_PAIRS:
+                quantise(ops[p])
         exponentials(N_PAIRS - 1)

@@ -25,11 +25,12 @@ GROUP_TILES = GROUP_PAIRS * PAIR_TILES
 GROUP_ROWS = GROUP_TILES * P
 N_GROUPS = BATCH // GROUP_ROWS
 N_PAIRS = BATCH // PAIR_ROWS
+ROUNDS = (4, 4, 4, 4)
+X_BUFS = 4
+M_BUFS = N_GROUPS
 
 E_MAX = 1.0e8 - 1.0
 
-ROUND = 4
-LOAD_AHEAD = 5
 
 FLOPS = 2 * BATCH * HID * FEAT * 4
 
@@ -42,8 +43,8 @@ def tile_slstmlayer_pa_t_kernel(
         consts = ctx.enter_context(tc.tile_pool(name="consts", bufs=1))
         raws = ctx.enter_context(tc.tile_pool(name="raws", bufs=5))
         grouped_pool = ctx.enter_context(tc.tile_pool(name="grouped_pool", bufs=2))
-        codes_pool = ctx.enter_context(tc.tile_pool(name="codes_pool", bufs=7))
-        gate_pool = ctx.enter_context(tc.tile_pool(name="gate_pool", bufs=6))
+        codes_pool = ctx.enter_context(tc.tile_pool(name="codes_pool", bufs=6))
+        gate_pool = ctx.enter_context(tc.tile_pool(name="gate_pool", bufs=5))
         arg_pool = ctx.enter_context(tc.tile_pool(name="arg_pool", bufs=6))
         m_t_pool = ctx.enter_context(tc.tile_pool(name="m_t_pool", bufs=3))
         psum = ctx.enter_context(tc.psum_pool(name="psum", bufs=2))
@@ -65,7 +66,7 @@ def tile_slstmlayer_pa_t_kernel(
         raw = {}
 
         def new_raw(name, g):
-            raw[name, g] = raws.tile([P, GROUP_TILES, FEAT], BF16, tag=name, name=name)
+            raw[name, g] = raws.tile([P, GROUP_TILES, FEAT], BF16, tag=name, name=name, bufs=M_BUFS if name == "m" else X_BUFS)
 
         def load_group(name, dram, g):
             new_raw(name, g)
@@ -78,7 +79,7 @@ def tile_slstmlayer_pa_t_kernel(
             )
 
         def load_weight(w, name):
-            tile = consts.tile([P, CHUNKS, FEAT], BF16, tag=name, name=name)
+            tile = arg_pool.tile([P, CHUNKS, FEAT], BF16, tag="args", name=name)
             nc.sync.dma_start(out=tile[:], in_=w.rearrange("(c p) k -> p c k", p=P))
             return tile
 
@@ -98,7 +99,7 @@ def tile_slstmlayer_pa_t_kernel(
             copy(out=words.rearrange("p (r u) -> p r u", u=2), in_=bank[:].rearrange("p u r -> p r u"))
 
         def new_operand(pool, name):
-            grouped = grouped_pool.tile([P, 8 * PAIR_ROWS], BF16, tag=name + "_grouped", name="grouped", align_bytes=64)
+            grouped = grouped_pool.tile([P, 8 * PAIR_ROWS], BF16, tag="w_grouped", name="grouped", align_bytes=64)
             codes = pool.tile([P, 2 * PAIR_ROWS], U32, tag=name + "_codes", name="codes", align_bytes=64)
             scales = pool.tile([P, 2 * PAIR_ROWS], U8, tag=name + "_scales", name="scales", align_bytes=64)
             return {"grouped": grouped, "codes": codes, "scales": scales}
@@ -107,6 +108,16 @@ def tile_slstmlayer_pa_t_kernel(
             nc.vector.quantize_mx(
                 out=op["codes"][:].bitcast(FP8X4), scales=op["scales"][:], in_=op["grouped"][:]
             )
+
+        def quantise_pair(s):
+            g, half = divmod(s, GROUP_PAIRS)
+            for part in range(2):
+                cols = slice((part * GROUP_PAIRS + half) * PAIR_ROWS, (part * GROUP_PAIRS + half + 1) * PAIR_ROWS)
+                nc.vector.quantize_mx(
+                    out=ops[g]["codes"][:, cols].bitcast(FP8X4),
+                    scales=ops[g]["scales"][:, cols],
+                    in_=grouped_rows[s][:, part * 4 * PAIR_ROWS : (part + 1) * 4 * PAIR_ROWS],
+                )
 
         def mx(out, lhs, lhs_cols, rhs, rhs_cols, start, stop):
             nc.tensor.matmul_mx(
@@ -122,14 +133,15 @@ def tile_slstmlayer_pa_t_kernel(
         weights = {}
         wbanks = {}
         ops = {}
+        grouped_rows = {}
         tr_banks = {}
         gates = {}
         f_banks = {}
         i_banks = {}
         s_banks = {}
         args = {}
-        X_COLS = slice(0, PAIR_ROWS)
-        H_COLS = slice(PAIR_ROWS, 2 * PAIR_ROWS)
+        X_COLS = slice(0, GROUP_ROWS)
+        H_COLS = slice(GROUP_ROWS, 2 * GROUP_ROWS)
 
         def weight_T(rows, name, tags):
             wbanks[name] = [transpose_rows(rows, 0, tags), transpose_rows(rows, PAIR_TILES, tags)]
@@ -140,50 +152,62 @@ def tile_slstmlayer_pa_t_kernel(
             for part in parts:
                 copy_out(weights[name]["grouped"], part, wbanks[name][part], copies[part])
 
-        def prep_T(s, parts=(0, 1)):
+        def prep_T(s, parts=(0, 1), tag="tr"):
             g, half = divmod(s, GROUP_PAIRS)
             for part in parts:
-                tr_banks[s, part] = transpose_rows(raw["xh"[part], g], half * PAIR_TILES, "tr")
+                tr_banks[s, part] = transpose_rows(raw["xh"[part], g], half * PAIR_TILES, tag)
 
         def prep_copy(s, copies, parts=(0, 1)):
-            if s not in ops:
-                ops[s] = new_operand(codes_pool, "act")
+            g = s // GROUP_PAIRS
+            if g not in ops:
+                codes = codes_pool.tile([P, 2 * GROUP_ROWS], U32, tag="codes", name="codes", align_bytes=64)
+                scales = codes_pool.tile([P, 2 * GROUP_ROWS], U8, tag="scales", name="scales", align_bytes=64)
+                ops[g] = {"codes": codes, "scales": scales}
+            if s not in grouped_rows:
+                grouped_rows[s] = grouped_pool.tile([P, 8 * PAIR_ROWS], BF16, tag="act_grouped", name="grouped", align_bytes=64)
             for part in parts:
-                copy_out(ops[s]["grouped"], part, tr_banks[s, part], copies[part])
+                copy_out(grouped_rows[s], part, tr_banks[s, part], copies[part])
 
         def f_T(s):
+            g, half = divmod(s, GROUP_PAIRS)
             f_banks[s] = []
-            for b in range(2):
-                bank = psum.tile([P, 2, PAIR_ROWS], F32, tag="pf", name="f_bank")
-                for j in range(2):
-                    cols = slice((2 * b + j) * P, (2 * b + j + 1) * P)
-                    mx(bank[:, j, :], weights["fx"], cols, ops[s], X_COLS, True, False)
-                    mx(bank[:, j, :], weights["fh"], cols, ops[s], H_COLS, False, True)
+            for c in (2 * half, 2 * half + 1):
+                bank = psum.tile([P, GROUP_ROWS], F32, tag="pf", name="f_bank")
+                cols = slice(c * P, (c + 1) * P)
+                mx(bank[:], weights["fx"], cols, ops[g], X_COLS, True, False)
+                mx(bank[:], weights["fh"], cols, ops[g], H_COLS, False, True)
                 f_banks[s].append(bank)
 
         def f_exp(s):
-            gates[s] = gate_pool.tile([P, CHUNKS, PAIR_ROWS], F32, tag="gate", name="gate")
-            for c in range(CHUNKS):
+            g, half = divmod(s, GROUP_PAIRS)
+            if half == 0:
+                gates[g] = gate_pool.tile([P, CHUNKS, GROUP_ROWS], F32, tag="gate", name="gate")
+            for j, bank in enumerate(f_banks[s]):
+                c = 2 * half + j
                 nc.scalar.activation(
-                    out=gates[s][:, c, :], in_=f_banks[s][c // 2][:, c % 2, :], func=ACT.Exp,
-                    bias=neg_bf[:, c : c + 1], scale=-1.0,
+                    out=gates[g][:, c, :], in_=bank[:], func=ACT.Exp, bias=neg_bf[:, c : c + 1], scale=-1.0
                 )
 
         def f_clamp(s):
-            for b in range(2):
-                flat = gates[s][:, 2 * b : 2 * b + 2, :].rearrange("p c b -> p (c b)")
+            g, half = divmod(s, GROUP_PAIRS)
+            for c in (2 * half, 2 * half + 1):
+                flat = gates[g][:, c, :]
                 nc.gpsimd.tensor_scalar(out=flat, in0=flat, scalar1=E_MAX, scalar2=0.0, op0=ALU.min, op1=ALU.max)
 
         def f_log(s):
-            flat = gates[s][:].rearrange("p c b -> p (c b)")
-            nc.scalar.activation(out=flat, in_=flat, func=ACT.Ln, bias=one[:], scale=1.0)
+            g, half = divmod(s, GROUP_PAIRS)
+            rows = gates[g][:, :, half * PAIR_ROWS : (half + 1) * PAIR_ROWS]
+            nc.scalar.activation(out=rows, in_=rows, func=ACT.Ln, bias=one[:], scale=1.0)
 
         def i_T(s):
+            g, half = divmod(s, GROUP_PAIRS)
             i_banks[s] = []
             for t in range(PAIR_TILES):
                 bank = psum.tile([P, HID], F32, tag="pi", name="i_bank")
-                mx(bank[:], ops[s], slice(t * P, (t + 1) * P), weights["ix"], slice(0, HID), True, False)
-                mx(bank[:], ops[s], slice(PAIR_ROWS + t * P, PAIR_ROWS + (t + 1) * P), weights["ih"], slice(0, HID), False, True)
+                row = half * PAIR_ROWS + t * P
+                mx(bank[:], ops[g], slice(row, row + P), weights["ix"], slice(0, HID), True, False)
+                row += GROUP_ROWS
+                mx(bank[:], ops[g], slice(row, row + P), weights["ih"], slice(0, HID), False, True)
                 i_banks[s].append(bank)
 
         def s_T(s):
@@ -194,7 +218,7 @@ def tile_slstmlayer_pa_t_kernel(
                 for c in range(CHUNKS):
                     nc.tensor.matmul(
                         out=bank[:, c * P : (c + 1) * P],
-                        lhsT=gates[s][:, c, t * P : (t + 1) * P],
+                        lhsT=gates[g][:, c, (half * PAIR_TILES + t) * P : (half * PAIR_TILES + t + 1) * P],
                         rhs=ident_f32[:],
                         is_transpose=True,
                         start=(c == 0),
@@ -262,93 +286,135 @@ def tile_slstmlayer_pa_t_kernel(
         load_pair("x", x, 1)
         load_pair("h", h_prev, 1)
         wix_raw = load_weight(Wi_x, "wix_raw")
-        wih_raw = load_weight(Wi_h, "wih_raw")
         load_group("x", x, 1)
         load_group("h", h_prev, 1)
+        wih_raw = load_weight(Wi_h, "wih_raw")
+        load_group("x", x, 2)
+        load_group("h", h_prev, 2)
         bi_all = consts.tile([P, HID], BF16, tag="bi_all")
         nc.sync.dma_start(out=bi_all[:], in_=b_i.partition_broadcast(P))
         load_group("m", m_prev, 0)
-        for g in range(2, LOAD_AHEAD):
-            load_group("x", x, g)
-            load_group("h", h_prev, g)
-            load_group("m", m_prev, g - 1)
+        load_group("x", x, 3)
+        load_group("h", h_prev, 3)
+        load_group("m", m_prev, 1)
 
-        prep_T(0, (0,))
-        weight_T(wfx_raw, "fx", "pi")
-        prep_T(0, (1,))
-        weight_T(wfh_raw, "fh", "ps")
-        prep_copy(0, (V, A), (0,))
-        weight_copy("fx", (A, V))
-        prep_copy(0, (V, A), (1,))
-        weight_copy("fh", (V, A))
-        quantise(weights["fx"])
-        quantise(ops[0])
-        bias_bank = psum.tile([P, P], BF16, tag="pf", name="bias_bank")
-        nc.tensor.transpose(bias_bank[:], bias_rows[:], ident_bf16[:])
-        neg_bf = consts.tile([P, CHUNKS], F32, tag="neg_bf")
-        nc.vector.tensor_scalar(out=neg_bf[:], in0=bias_bank[:, 0:CHUNKS], scalar1=-1.0, scalar2=None, op0=ALU.mult)
-        quantise(weights["fh"])
+        def load_activations(g):
+            if g < N_GROUPS:
+                load_group("x", x, g)
+                load_group("h", h_prev, g)
+                load_group("m", m_prev, g - 2)
+            if g == N_GROUPS - 1:
+                load_group("m", m_prev, g - 1)
+                load_group("m", m_prev, g)
 
         def forget(s):
             f_T(s)
             f_exp(s)
             f_clamp(s)
 
-        prep_T(1)
-        for s in range(ROUND):
-            prep_copy(s + 1, (V, A))
-            if s == 1:
-                weight_copy("ix", (V, V))
-            if s == 2:
-                weight_copy("ih", (V, V))
-            forget(s)
-            prep_T(s + 2)
-            quantise(ops[s + 1])
-            if s == 0:
-                weight_T(wix_raw, "ix", "pi")
-            if s == 1:
-                weight_T(wih_raw, "ih", "ps")
-                quantise(weights["ix"])
-            if s == 2:
-                quantise(weights["ih"])
+        prep_T(0, (0,))
+        weight_T(wfx_raw, "fx", "pi")
+        prep_T(0, (1,))
+        weight_T(wfh_raw, "fh", "ps")
+        bias_bank = psum.tile([P, P], BF16, tag="pf", name="bias_bank")
+        nc.tensor.transpose(bias_bank[:], bias_rows[:], ident_bf16[:])
+        prep_copy(0, (V, A), (0,))
+        prep_T(1, (0,))
+        weight_copy("fx", (A, V))
+        prep_copy(0, (V, A), (1,))
+        prep_T(1, (1,))
+        load_activations(X_BUFS)
+        weight_copy("fh", (V, A))
+        quantise(weights["fx"])
+        prep_copy(1, (V, A))
+        quantise_pair(0)
+        quantise(weights["fh"])
+        neg_bf = consts.tile([P, CHUNKS], F32, tag="neg_bf")
+        nc.vector.tensor_scalar(out=neg_bf[:], in0=bias_bank[:, 0:CHUNKS], scalar1=-1.0, scalar2=None, op0=ALU.mult)
+        quantise_pair(1)
+        weight_T(wix_raw, "ix", "pi")
+        prep_T(2, tag="ps")
+        weight_copy("ix", (A, A))
+        prep_T(3)
+        load_activations(X_BUFS + 1)
+        prep_copy(2, (V, V))
+        prep_copy(3, (V, A))
+        forget(0)
+        quantise_pair(2)
+        forget(1)
+        quantise_pair(3)
+        weight_T(wih_raw, "ih", "pi")
+        quantise(weights["ix"])
+        if ROUNDS[0] > 2:
+            forget(2)
+        weight_copy("ih", (V, V))
+        if ROUNDS[0] > 2:
+            forget(3)
+        prep_T(4)
+        quantise(weights["ih"])
+        if ROUNDS[0] > 2:
+            prep_copy(4, (V, V))
         i_T(0)
-        for s in range(ROUND):
+        if ROUNDS[0] > 2:
+            prep_T(5)
+            load_activations(X_BUFS + 2)
+            quantise_pair(4)
+            prep_copy(5, (V, V))
+        for s in range(ROUNDS[0]):
             f_log(s)
         s_T(0)
+        if ROUNDS[0] > 2:
+            prep_T(6)
+            quantise_pair(5)
 
-        for k in range(N_PAIRS):
-            g = k // GROUP_PAIRS + LOAD_AHEAD
-            if k % GROUP_PAIRS == 0 and g <= N_GROUPS:
-                load_group("m", m_prev, g - 1)
-                if g < N_GROUPS:
-                    load_group("x", x, g)
-                    load_group("h", h_prev, g)
-            e = k + ROUND
-            chain_i(k)
-            if e < N_PAIRS:
-                f_T(e)
-                f_exp(e)
-                f_clamp(e)
-            chain_m(k)
-            chain_g(k)
-            if k + 1 < N_PAIRS:
-                i_T(k + 1)
-            chain_f(k)
-            first, last = k % ROUND == 0, k % ROUND == ROUND - 1 and e < N_PAIRS
-            if first and k > 0:
-                exponentials(k - 2)
-            if k > 0 and not last:
-                exponentials(k - 1)
-            p = e + 1
-            if p < N_PAIRS:
-                prep_copy(p, (V, V))
-            if last:
-                for s in range(k + 1, k + 1 + ROUND):
-                    f_log(s)
-            if k + 1 < N_PAIRS:
-                s_T(k + 1)
-            if p + 1 < N_PAIRS:
-                prep_T(p + 1)
-            if p < N_PAIRS:
-                quantise(ops[p])
-        exponentials(N_PAIRS - 1)
+        sent = 0
+        start = 0
+        unit = ROUNDS[0]
+        p = unit + 2
+        for r, n in enumerate(ROUNDS):
+            end = start + n
+            more = ROUNDS[r + 1] if r + 1 < len(ROUNDS) else 0
+            reach = [1 if q == 0 else (more * (q + 1) + n - 1) // n for q in range(n)] + [more + 1]
+            for q in range(n):
+                k = start + q
+                units = list(range(unit, end + reach[q])) if more else []
+                unit += len(units)
+                last = more and q == n - 1
+                goal = min(N_PAIRS, end + reach[q + 1] + 1 + (1 if last else 0))
+                preps = list(range(p, goal)) if more else []
+                p += len(preps)
+                share = r == 0 and not last and len(preps) > 0
+                if share:
+                    prep_copy(preps[0], (V, A), (1,))
+                chain_i(k)
+                if units:
+                    forget(units[0])
+                chain_m(k)
+                chain_g(k)
+                if k + 1 < N_PAIRS:
+                    i_T(k + 1)
+                chain_f(k)
+                outs = 0 if last else 2 if q == 0 or not more else 1
+                while outs and sent < k:
+                    exponentials(sent)
+                    sent += 1
+                    outs -= 1
+                for s in units[1:]:
+                    forget(s)
+                for j, s in enumerate(preps):
+                    prep_copy(s, (V, V), (0,) if share and j == 0 else (0, 1))
+                    if not last and j == 0:
+                        s_T(k + 1)
+                    if s + 1 < N_PAIRS:
+                        prep_T(s + 1)
+                        if s % GROUP_PAIRS == 0:
+                            load_activations(s // GROUP_PAIRS + X_BUFS)
+                    quantise_pair(s)
+                if last:
+                    for s in range(end, end + more):
+                        f_log(s)
+                if k + 1 < N_PAIRS and (last or not preps):
+                    s_T(k + 1)
+            start = end
+        for s in range(sent, N_PAIRS):
+            exponentials(s)

@@ -168,11 +168,11 @@ def tile_slstmlayer_pa_t_kernel(
             for part in parts:
                 copy_out(grouped_rows[s], part, tr_banks[s, part], copies[part])
 
-        def f_T(s):
+        def f_T(s, tag="pf"):
             g, half = divmod(s, GROUP_PAIRS)
             f_banks[s] = []
             for c in (2 * half, 2 * half + 1):
-                bank = psum.tile([P, GROUP_ROWS], F32, tag="pf", name="f_bank")
+                bank = psum.tile([P, GROUP_ROWS], F32, tag=tag, name="f_bank")
                 cols = slice(c * P, (c + 1) * P)
                 mx(bank[:], weights["fx"], cols, ops[g], X_COLS, True, False)
                 mx(bank[:], weights["fh"], cols, ops[g], H_COLS, False, True)
@@ -270,6 +270,11 @@ def tile_slstmlayer_pa_t_kernel(
         bias_rows = consts.tile([P, P], BF16, tag="bias_rows")
         nc.vector.memset(bias_rows[:], 0.0)
         nc.scalar.dma_start(out=bias_rows[0:CHUNKS, :], in_=b_f.rearrange("(c p) -> c p", p=P))
+        bi_row = consts.tile([P, HID], BF16, tag="bi_row")
+        nc.vector.memset(bi_row[:], 0.0)
+        nc.scalar.dma_start(out=bi_row[0:1, :], in_=b_i.rearrange("(a k) -> a k", a=1))
+        ones = consts.tile([P, P], BF16, tag="ones")
+        nc.vector.memset(ones[:], 1.0)
         one = consts.tile([P, 1], F32, tag="one")
         nc.vector.memset(one[:], 1.0)
         warm = consts.tile([P, 1], F32, tag="warm")
@@ -291,8 +296,6 @@ def tile_slstmlayer_pa_t_kernel(
         wih_raw = load_weight(Wi_h, "wih_raw")
         load_group("x", x, 2)
         load_group("h", h_prev, 2)
-        bi_all = consts.tile([P, HID], BF16, tag="bi_all")
-        nc.sync.dma_start(out=bi_all[:], in_=b_i.partition_broadcast(P))
         load_group("m", m_prev, 0)
         load_group("x", x, 3)
         load_group("h", h_prev, 3)
@@ -307,8 +310,8 @@ def tile_slstmlayer_pa_t_kernel(
                 load_group("m", m_prev, g - 1)
                 load_group("m", m_prev, g)
 
-        def forget(s):
-            f_T(s)
+        def forget(s, tag="pf"):
+            f_T(s, tag)
             f_exp(s)
             f_clamp(s)
 
@@ -335,37 +338,36 @@ def tile_slstmlayer_pa_t_kernel(
         weight_T(wix_raw, "ix", "pi")
         prep_T(2, tag="ps")
         weight_copy("ix", (A, A))
+        forget(0)
+        prep_copy(2, (V, V))
         prep_T(3)
         load_activations(X_BUFS + 1)
-        prep_copy(2, (V, V))
-        prep_copy(3, (V, A))
-        forget(0)
         quantise_pair(2)
-        forget(1)
+        prep_copy(3, (V, V))
+        forget(1, "ps")
         quantise_pair(3)
-        weight_T(wih_raw, "ih", "pi")
         quantise(weights["ix"])
-        if ROUNDS[0] > 2:
-            forget(2)
+        weight_T(wih_raw, "ih", "pi")
+        bi_bank = psum.tile([P, HID], F32, tag="tr", name="bi_bank")
+        nc.tensor.matmul(out=bi_bank[:], lhsT=ones[:], rhs=bi_row[:], start=True, stop=True)
+        bi_all = consts.tile([P, HID], BF16, tag="bi_all")
+        nc.scalar.copy(out=bi_all[:], in_=bi_bank[:])
+        forget(2)
         weight_copy("ih", (V, V))
-        if ROUNDS[0] > 2:
-            forget(3)
+        forget(3, "ps")
         prep_T(4)
         quantise(weights["ih"])
-        if ROUNDS[0] > 2:
-            prep_copy(4, (V, V))
+        prep_copy(4, (V, V))
         i_T(0)
-        if ROUNDS[0] > 2:
-            prep_T(5)
-            load_activations(X_BUFS + 2)
-            quantise_pair(4)
-            prep_copy(5, (V, V))
+        quantise_pair(4)
+        prep_T(5)
+        load_activations(X_BUFS + 2)
         for s in range(ROUNDS[0]):
             f_log(s)
         s_T(0)
-        if ROUNDS[0] > 2:
-            prep_T(6)
-            quantise_pair(5)
+        prep_copy(5, (V, V))
+        prep_T(6)
+        quantise_pair(5)
 
         sent = 0
         start = 0

@@ -27,6 +27,7 @@ N_GROUPS = BATCH // GROUP_ROWS
 N_PAIRS = BATCH // PAIR_ROWS
 ROUNDS = (4, 4, 4, 4)
 X_BUFS = 4
+HOLD = 1
 M_BUFS = N_GROUPS
 
 E_MAX = 1.0e8 - 1.0
@@ -396,7 +397,7 @@ def tile_slstmlayer_pa_t_kernel(
                 if k + 1 < N_PAIRS:
                     i_T(k + 1)
                 chain_f(k)
-                outs = 0 if last else 2 if q == 0 or not more else 1
+                outs = 0 if last else (2 if q >= HOLD else 0) if not more else 2 if q == 0 else 1
                 while outs and sent < k:
                     exponentials(sent)
                     sent += 1

@@ -248,9 +248,7 @@ def tile_slstmlayer_pa_t_kernel(
             nc.sync.dma_start(out=pair_view(out_0, s), in_=m_ts[s][:].rearrange("p (t k) -> p t k", t=PAIR_TILES))
 
         def chain_g(s):
-            for t in range(PAIR_TILES):
-                cols = slice(t * HID, (t + 1) * HID)
-                nc.gpsimd.tensor_tensor(out=args[s][:, 0, cols], in0=args[s][:, 0, cols], in1=m_ts[s][:, cols], op=ALU.subtract)
+            nc.gpsimd.tensor_tensor(out=args[s][:, 0, :], in0=args[s][:, 0, :], in1=m_ts[s][:], op=ALU.subtract)
 
         def chain_f(s):
             for t in range(PAIR_TILES):
@@ -383,7 +381,7 @@ def tile_slstmlayer_pa_t_kernel(
                 units = list(range(unit, end + reach[q])) if more else []
                 unit += len(units)
                 last = more and q == n - 1
-                goal = min(N_PAIRS, end + reach[q + 1] + 1 + (1 if last else 0))
+                goal = min(N_PAIRS, end + reach[q + 1] + 1 + 0)
                 preps = list(range(p, goal)) if more else []
                 p += len(preps)
                 share = r == 0 and not last and len(preps) > 0

@@ -51,6 +51,8 @@ def tile_slstmlayer_pa_t_kernel(
         psum = ctx.enter_context(tc.psum_pool(name="psum", bufs=2))
         ctx.enter_context(tc.manual_schedule())
 
+        idle_rows = consts.tile([P, HID], BF16, tag="idle_rows")
+        nc.vector.memset(idle_rows[:], 0.0)
         ident_f32 = consts.tile([P, P], F32, tag="ident_f32")
         make_identity(nc, ident_f32[:])
         ident_bf16 = consts.tile([P, P], BF16, tag="ident_bf16")
@@ -314,7 +316,14 @@ def tile_slstmlayer_pa_t_kernel(
             f_exp(s)
             f_clamp(s)
 
+        def keep_warm(count):
+            for j in range(count):
+                bank = psum.tile([P, HID], F32, tag="pf", name="idle_bank")
+                nc.tensor.matmul(out=bank[:], lhsT=idle_rows[:, 0:P], rhs=idle_rows[:], start=True, stop=True)
+
+        keep_warm(3)
         prep_T(0, (0,))
+        keep_warm(1)
         weight_T(wfx_raw, "fx", "pi")
         prep_T(0, (1,))
         weight_T(wfh_raw, "fh", "ps")
@@ -334,8 +343,12 @@ def tile_slstmlayer_pa_t_kernel(
         neg_bf = consts.tile([P, CHUNKS], F32, tag="neg_bf")
         nc.vector.tensor_scalar(out=neg_bf[:], in0=bias_bank[:, 0:CHUNKS], scalar1=-1.0, scalar2=None, op0=ALU.mult)
         quantise_pair(1)
+        keep_warm(1)
         weight_T(wix_raw, "ix", "pi")
-        prep_T(2, tag="ps")
+        keep_warm(1)
+        prep_T(2, (0,), tag="ps")
+        keep_warm(1)
+        prep_T(2, (1,), tag="ps")
         weight_copy("ix", (A, A))
         forget(0)
         prep_copy(2, (V, V))

@@ -28,6 +28,23 @@ N_PAIRS = BATCH // PAIR_ROWS
 ROUNDS = (4, 4, 4, 4)
 X_BUFS = 4
 HOLD = 1
+S_MODE = 1
+EXTRA = 2
+S0_AT = 1
+ORDER = "imfcgFekLISpxq"
+LAST_ORDER = "iFmcxefIkgLpqS"
+BACKLOG = 0
+LEAD = 4
+I_LEAD = 0
+SHARE = 6
+X_DUE = 0
+X_LAST = 1
+X_TWO = 2
+G_SPLIT = 2
+GATE_BUFS = 6
+ARG_BUFS = 5
+CODE_BUFS = 5
+UNIT_EARLY = 0
 M_BUFS = N_GROUPS
 
 E_MAX = 1.0e8 - 1.0
@@ -44,9 +61,9 @@ def tile_slstmlayer_pa_t_kernel(
         consts = ctx.enter_context(tc.tile_pool(name="consts", bufs=1))
         raws = ctx.enter_context(tc.tile_pool(name="raws", bufs=5))
         grouped_pool = ctx.enter_context(tc.tile_pool(name="grouped_pool", bufs=2))
-        codes_pool = ctx.enter_context(tc.tile_pool(name="codes_pool", bufs=6))
-        gate_pool = ctx.enter_context(tc.tile_pool(name="gate_pool", bufs=5))
-        arg_pool = ctx.enter_context(tc.tile_pool(name="arg_pool", bufs=6))
+        codes_pool = ctx.enter_context(tc.tile_pool(name="codes_pool", bufs=CODE_BUFS))
+        gate_pool = ctx.enter_context(tc.tile_pool(name="gate_pool", bufs=GATE_BUFS))
+        arg_pool = ctx.enter_context(tc.tile_pool(name="arg_pool", bufs=ARG_BUFS))
         m_t_pool = ctx.enter_context(tc.tile_pool(name="m_t_pool", bufs=3))
         psum = ctx.enter_context(tc.psum_pool(name="psum", bufs=2))
         ctx.enter_context(tc.manual_schedule())
@@ -215,9 +232,14 @@ def tile_slstmlayer_pa_t_kernel(
 
         def s_T(s):
             g, half = divmod(s, GROUP_PAIRS)
-            s_banks[s] = []
-            for t in range(PAIR_TILES):
-                bank = psum.tile([P, HID], F32, tag="ps", name="s_bank")
+            s_banks[s] = [psum.tile([P, HID], F32, tag="ps", name="s_bank") for t in range(PAIR_TILES)]
+
+            def minus_m(t):
+                nc.tensor.matmul(
+                    out=s_banks[s][t][:], lhsT=neg_ident[:], rhs=raw["m", g][:, half * PAIR_TILES + t, :], start=False, stop=True
+                )
+
+            for t, bank in enumerate(s_banks[s]):
                 for c in range(CHUNKS):
                     nc.tensor.matmul(
                         out=bank[:, c * P : (c + 1) * P],
@@ -227,10 +249,11 @@ def tile_slstmlayer_pa_t_kernel(
                         start=(c == 0),
                         stop=False,
                     )
-                nc.tensor.matmul(
-                    out=bank[:], lhsT=neg_ident[:], rhs=raw["m", g][:, half * PAIR_TILES + t, :], start=False, stop=True
-                )
-                s_banks[s].append(bank)
+                if S_MODE == 0:
+                    minus_m(t)
+            if S_MODE == 1:
+                for t in range(PAIR_TILES):
+                    minus_m(t)
 
         m_ts = {}
 
@@ -250,7 +273,9 @@ def tile_slstmlayer_pa_t_kernel(
             nc.sync.dma_start(out=pair_view(out_0, s), in_=m_ts[s][:].rearrange("p (t k) -> p t k", t=PAIR_TILES))
 
         def chain_g(s):
-            nc.gpsimd.tensor_tensor(out=args[s][:, 0, :], in0=args[s][:, 0, :], in1=m_ts[s][:], op=ALU.subtract)
+            for j in range(G_SPLIT):
+                cols = slice(j * PAIR_TILES * HID // G_SPLIT, (j + 1) * PAIR_TILES * HID // G_SPLIT)
+                nc.gpsimd.tensor_tensor(out=args[s][:, 0, cols], in0=args[s][:, 0, cols], in1=m_ts[s][:, cols], op=ALU.subtract)
 
         def chain_f(s):
             for t in range(PAIR_TILES):
@@ -291,9 +316,9 @@ def tile_slstmlayer_pa_t_kernel(
         wfh_raw = load_weight(Wf_h, "wfh_raw")
         load_pair("x", x, 1)
         load_pair("h", h_prev, 1)
-        wix_raw = load_weight(Wi_x, "wix_raw")
         load_group("x", x, 1)
         load_group("h", h_prev, 1)
+        wix_raw = load_weight(Wi_x, "wix_raw")
         wih_raw = load_weight(Wi_h, "wih_raw")
         load_group("x", x, 2)
         load_group("h", h_prev, 2)
@@ -302,7 +327,12 @@ def tile_slstmlayer_pa_t_kernel(
         load_group("h", h_prev, 3)
         load_group("m", m_prev, 1)
 
+        loaded = set()
+
         def load_activations(g):
+            if g in loaded:
+                return
+            loaded.add(g)
             if g < N_GROUPS:
                 load_group("x", x, g)
                 load_group("h", h_prev, g)
@@ -323,112 +353,159 @@ def tile_slstmlayer_pa_t_kernel(
 
         keep_warm(3)
         prep_T(0, (0,))
-        keep_warm(1)
         weight_T(wfx_raw, "fx", "pi")
         prep_T(0, (1,))
         weight_T(wfh_raw, "fh", "ps")
-        bias_bank = psum.tile([P, P], BF16, tag="pf", name="bias_bank")
-        nc.tensor.transpose(bias_bank[:], bias_rows[:], ident_bf16[:])
         prep_copy(0, (V, A), (0,))
-        prep_T(1, (0,))
         weight_copy("fx", (A, V))
+        prep_T(1, (0,))
         prep_copy(0, (V, A), (1,))
-        prep_T(1, (1,))
-        load_activations(X_BUFS)
         weight_copy("fh", (V, A))
         quantise(weights["fx"])
-        prep_copy(1, (V, A))
+        prep_T(1, (1,))
+        prep_copy(1, (V, A), (0,))
         quantise_pair(0)
         quantise(weights["fh"])
+        prep_copy(1, (V, A), (1,))
+        quantise_pair(1)
+        bias_bank = psum.tile([P, P], BF16, tag="pf", name="bias_bank")
+        nc.tensor.transpose(bias_bank[:], bias_rows[:], ident_bf16[:])
         neg_bf = consts.tile([P, CHUNKS], F32, tag="neg_bf")
         nc.vector.tensor_scalar(out=neg_bf[:], in0=bias_bank[:, 0:CHUNKS], scalar1=-1.0, scalar2=None, op0=ALU.mult)
-        quantise_pair(1)
-        keep_warm(1)
-        weight_T(wix_raw, "ix", "pi")
-        keep_warm(1)
-        prep_T(2, (0,), tag="ps")
-        keep_warm(1)
-        prep_T(2, (1,), tag="ps")
-        weight_copy("ix", (A, A))
+        prep_T(2, (0,), tag="pi")
+        prep_T(2, (1,), tag="pi")
+        prep_copy(2, (V, A))
+        prep_T(3, (0,), tag="tr")
+        prep_T(3, (1,), tag="tr")
+        prep_copy(3, (V, A))
         forget(0)
-        prep_copy(2, (V, V))
-        prep_T(3)
-        load_activations(X_BUFS + 1)
         quantise_pair(2)
-        prep_copy(3, (V, V))
-        forget(1, "ps")
         quantise_pair(3)
+        load_activations(X_BUFS)
+        forget(1, "ps")
+        load_activations(X_BUFS + 1)
+        weight_T(wix_raw, "ix", "pi")
+        forget(2)
+        weight_T(wih_raw, "ih", "tr")
+        forget(3, "ps")
+        weight_copy("ix", (V, V))
+        weight_copy("ih", (V, V))
         quantise(weights["ix"])
-        weight_T(wih_raw, "ih", "pi")
-        bi_bank = psum.tile([P, HID], F32, tag="tr", name="bi_bank")
+        bi_bank = psum.tile([P, HID], F32, tag="pi", name="bi_bank")
         nc.tensor.matmul(out=bi_bank[:], lhsT=ones[:], rhs=bi_row[:], start=True, stop=True)
         bi_all = consts.tile([P, HID], BF16, tag="bi_all")
         nc.scalar.copy(out=bi_all[:], in_=bi_bank[:])
-        forget(2)
-        weight_copy("ih", (V, V))
-        forget(3, "ps")
-        prep_T(4)
         quantise(weights["ih"])
-        prep_copy(4, (V, V))
+        prep_T(4)
         i_T(0)
-        quantise_pair(4)
-        prep_T(5)
-        load_activations(X_BUFS + 2)
         for s in range(ROUNDS[0]):
             f_log(s)
-        s_T(0)
-        prep_copy(5, (V, V))
-        prep_T(6)
-        quantise_pair(5)
+        for s in range(ROUNDS[0], ROUNDS[0] + EXTRA):
+            prep_copy(s, (V, V))
+            if s == ROUNDS[0] + S0_AT:
+                s_T(0)
+            prep_T(s + 1)
+            if s % GROUP_PAIRS == 0:
+                load_activations(s // GROUP_PAIRS + X_BUFS)
+            quantise_pair(s)
+        if S0_AT >= EXTRA:
+            s_T(0)
 
+        for s in range(I_LEAD):
+            chain_i(s)
+            i_T(s + 1)
+        todo = list(range(ROUNDS[0], N_PAIRS))
+        quantised = set(range(ROUNDS[0] + EXTRA))
+        copied = set(quantised)
+        transposed = ROUNDS[0] + 3
+        waiting = []
+        logged = ROUNDS[0]
         sent = 0
-        start = 0
-        unit = ROUNDS[0]
-        p = unit + 2
-        for r, n in enumerate(ROUNDS):
-            end = start + n
-            more = ROUNDS[r + 1] if r + 1 < len(ROUNDS) else 0
-            reach = [1 if q == 0 else (more * (q + 1) + n - 1) // n for q in range(n)] + [more + 1]
-            for q in range(n):
-                k = start + q
-                units = list(range(unit, end + reach[q])) if more else []
-                unit += len(units)
-                last = more and q == n - 1
-                goal = min(N_PAIRS, end + reach[q + 1] + 1 + 0)
-                preps = list(range(p, goal)) if more else []
-                p += len(preps)
-                share = r == 0 and not last and len(preps) > 0
-                if share:
-                    prep_copy(preps[0], (V, A), (1,))
-                chain_i(k)
-                if units:
-                    forget(units[0])
-                chain_m(k)
-                chain_g(k)
-                if k + 1 < N_PAIRS:
-                    i_T(k + 1)
-                chain_f(k)
-                outs = 0 if last else (2 if q >= HOLD else 0) if not more else 2 if q == 0 else 1
-                while outs and sent < k:
-                    exponentials(sent)
-                    sent += 1
-                    outs -= 1
-                for s in units[1:]:
-                    forget(s)
-                for j, s in enumerate(preps):
-                    prep_copy(s, (V, V), (0,) if share and j == 0 else (0, 1))
-                    if not last and j == 0:
+        r = 1
+        last_due = 0
+        for k in range(N_PAIRS):
+            n = ROUNDS[r] if r < len(ROUNDS) else 0
+            log_step = max(0, logged - 1 - BACKLOG)
+            due = n > 0 and k >= log_step
+            left = logged + n - (todo[0] if todo else N_PAIRS)
+            steps_left = max(1, log_step - k + 1)
+            units = []
+            if n and k <= log_step:
+                count = left if due else -(-left // steps_left) if UNIT_EARLY else left // steps_left
+                units = todo[:count]
+                todo = todo[count:]
+            elif not n:
+                units = []
+            goal = min(N_PAIRS, (units[-1] if units else (todo[0] - 1 if todo else N_PAIRS - 1)) // GROUP_PAIRS * GROUP_PAIRS + GROUP_PAIRS)
+            preps = []
+            nxt = max(copied) + 1
+            want = max(goal, min(N_PAIRS, max(copied) + 2)) if todo or units else N_PAIRS
+            cap = min(N_PAIRS, (units[-1] if units else logged + n - 1) + 1 + LEAD + 2)
+            while nxt < min(want, max(cap, goal)):
+                preps.append(nxt)
+                copied.add(nxt)
+                nxt += 1
+            share = k < SHARE
+            for a in LAST_ORDER if due else ORDER:
+                if a == "c":
+                    for s in preps:
+                        prep_copy(s, (V, A if share else V))
+                        waiting.append(s)
+                        if s != preps[-1] and s + 1 < N_PAIRS:
+                            prep_T(s + 1)
+                            if s % GROUP_PAIRS == 0:
+                                load_activations(s // GROUP_PAIRS + X_BUFS)
+                elif a == "p":
+                    for s in preps[-1:]:
+                        if s + 1 < N_PAIRS:
+                            prep_T(s + 1)
+                            if s % GROUP_PAIRS == 0:
+                                load_activations(s // GROUP_PAIRS + X_BUFS)
+                elif a == "q":
+                    for s in waiting:
+                        quantise_pair(s)
+                        quantised.add(s)
+                    waiting = []
+                elif a == "i":
+                    if k + I_LEAD < N_PAIRS:
+                        chain_i(k + I_LEAD)
+                elif a == "I":
+                    if k + I_LEAD + 1 < N_PAIRS:
+                        i_T(k + I_LEAD + 1)
+                elif a == "m":
+                    chain_m(k)
+                elif a == "g":
+                    chain_g(k)
+                elif a == "f":
+                    chain_f(k)
+                elif a == "S":
+                    if k + 1 < N_PAIRS:
                         s_T(k + 1)
-                    if s + 1 < N_PAIRS:
-                        prep_T(s + 1)
-                        if s % GROUP_PAIRS == 0:
-                            load_activations(s // GROUP_PAIRS + X_BUFS)
-                    quantise_pair(s)
-                if last:
-                    for s in range(end, end + more):
-                        f_log(s)
-                if k + 1 < N_PAIRS and (last or not preps):
-                    s_T(k + 1)
-            start = end
+                elif a == "F":
+                    for s in units:
+                        assert s | 1 in quantised and s & ~1 in quantised
+                        f_T(s)
+                        if len(units) > 1:
+                            f_exp(s)
+                            f_clamp(s)
+                elif a == "e":
+                    if len(units) == 1:
+                        f_exp(units[0])
+                elif a == "k":
+                    if len(units) == 1:
+                        f_clamp(units[0])
+                elif a == "x":
+                    outs = X_LAST if due and r == len(ROUNDS) - 1 else 0 if due and not X_DUE else (2 if k >= N_PAIRS - ROUNDS[-1] + HOLD else 0) if not n else 2 if r > 1 and k <= last_due + X_TWO else 1
+                    while outs and sent < k:
+                        exponentials(sent)
+                        sent += 1
+                        outs -= 1
+                elif a == "L":
+                    if due:
+                        for s in range(logged, logged + n):
+                            f_log(s)
+                        logged += n
+                        r += 1
+                        last_due = k
         for s in range(sent, N_PAIRS):
             exponentials(s)

@@ -28,23 +28,25 @@ N_PAIRS = BATCH // PAIR_ROWS
 ROUNDS = (4, 4, 4, 4)
 X_BUFS = 4
 HOLD = 1
-S_MODE = 1
+S_MODE = 0
 EXTRA = 2
 S0_AT = 1
-ORDER = "imfcgFekLISpxq"
-LAST_ORDER = "iFmcxefIkgLpqS"
+ORDER = "icmfFegIkLpSxq"
+LAST_ORDER = "FxceipkqmfLIjSg"
 BACKLOG = 0
-LEAD = 4
-I_LEAD = 0
-SHARE = 6
-X_DUE = 0
-X_LAST = 1
-X_TWO = 2
+LEAD = 3
+I_AHEAD = 1
+I_LAST = 1
+A_BUFS = 3
+SHARE = 3
+X_DUE = 1
+X_LAST = 0
+X_TWO = 0
 G_SPLIT = 2
 GATE_BUFS = 6
-ARG_BUFS = 5
-CODE_BUFS = 5
-UNIT_EARLY = 0
+ARG_BUFS = 4
+CODE_BUFS = 6
+UNIT_EARLY = 1
 M_BUFS = N_GROUPS
 
 E_MAX = 1.0e8 - 1.0
@@ -64,6 +66,7 @@ def tile_slstmlayer_pa_t_kernel(
         codes_pool = ctx.enter_context(tc.tile_pool(name="codes_pool", bufs=CODE_BUFS))
         gate_pool = ctx.enter_context(tc.tile_pool(name="gate_pool", bufs=GATE_BUFS))
         arg_pool = ctx.enter_context(tc.tile_pool(name="arg_pool", bufs=ARG_BUFS))
+        a_pool = ctx.enter_context(tc.tile_pool(name="a_pool", bufs=A_BUFS))
         m_t_pool = ctx.enter_context(tc.tile_pool(name="m_t_pool", bufs=3))
         psum = ctx.enter_context(tc.psum_pool(name="psum", bufs=2))
         ctx.enter_context(tc.manual_schedule())
@@ -256,26 +259,28 @@ def tile_slstmlayer_pa_t_kernel(
                     minus_m(t)
 
         m_ts = {}
+        a_tiles = {}
 
         def chain_i(s):
+            a_tiles[s] = a_pool.tile([P, PAIR_TILES * HID], F32, tag="a_tile", name="a_tile")
+            for t in range(PAIR_TILES):
+                cols = slice(t * HID, (t + 1) * HID)
+                nc.vector.tensor_tensor(out=a_tiles[s][:, cols], in0=i_banks[s][t][:], in1=bi_all[:], op=ALU.add)
+
+        def chain_m(s):
             args[s] = arg_pool.tile([P, 2, PAIR_TILES * HID], F32, tag="args", name="args")
             m_ts[s] = m_t_pool.tile([P, PAIR_TILES * HID], F32, tag="m_t", name="m_t")
             for t in range(PAIR_TILES):
                 cols = slice(t * HID, (t + 1) * HID)
-                nc.vector.tensor_tensor(out=args[s][:, 0, cols], in0=i_banks[s][t][:], in1=bi_all[:], op=ALU.add)
-
-        def chain_m(s):
-            for t in range(PAIR_TILES):
-                cols = slice(t * HID, (t + 1) * HID)
                 nc.vector.scalar_tensor_tensor(
-                    out=m_ts[s][:, cols], in0=s_banks[s][t][:], scalar=-1.0, in1=args[s][:, 0, cols], op0=ALU.mult, op1=ALU.max
+                    out=m_ts[s][:, cols], in0=s_banks[s][t][:], scalar=-1.0, in1=a_tiles[s][:, cols], op0=ALU.mult, op1=ALU.max
                 )
             nc.sync.dma_start(out=pair_view(out_0, s), in_=m_ts[s][:].rearrange("p (t k) -> p t k", t=PAIR_TILES))
 
         def chain_g(s):
             for j in range(G_SPLIT):
                 cols = slice(j * PAIR_TILES * HID // G_SPLIT, (j + 1) * PAIR_TILES * HID // G_SPLIT)
-                nc.gpsimd.tensor_tensor(out=args[s][:, 0, cols], in0=args[s][:, 0, cols], in1=m_ts[s][:, cols], op=ALU.subtract)
+                nc.gpsimd.tensor_tensor(out=args[s][:, 0, cols], in0=a_tiles[s][:, cols], in1=m_ts[s][:, cols], op=ALU.subtract)
 
         def chain_f(s):
             for t in range(PAIR_TILES):
@@ -411,9 +416,6 @@ def tile_slstmlayer_pa_t_kernel(
         if S0_AT >= EXTRA:
             s_T(0)
 
-        for s in range(I_LEAD):
-            chain_i(s)
-            i_T(s + 1)
         todo = list(range(ROUNDS[0], N_PAIRS))
         quantised = set(range(ROUNDS[0] + EXTRA))
         copied = set(quantised)
@@ -467,11 +469,17 @@ def tile_slstmlayer_pa_t_kernel(
                         quantised.add(s)
                     waiting = []
                 elif a == "i":
-                    if k + I_LEAD < N_PAIRS:
-                        chain_i(k + I_LEAD)
+                    if k not in a_tiles:
+                        chain_i(k)
                 elif a == "I":
-                    if k + I_LEAD + 1 < N_PAIRS:
-                        i_T(k + I_LEAD + 1)
+                    if k + 1 < N_PAIRS and k + 1 not in i_banks:
+                        i_T(k + 1)
+                elif a == "j":
+                    for s in range(k + 1, min(N_PAIRS, k + 1 + (I_AHEAD if r < len(ROUNDS) - 1 else I_LAST))):
+                        if s not in a_tiles:
+                            chain_i(s)
+                            if s + 1 < N_PAIRS:
+                                i_T(s + 1)
                 elif a == "m":
                     chain_m(k)
                 elif a == "g":

@@ -31,23 +31,25 @@ HOLD = 1
 S_MODE = 0
 EXTRA = 2
 S0_AT = 1
-ORDER = "icmfFegIkLpSxq"
-LAST_ORDER = "FxceipkqmfLIjSg"
+ORDER = "icFemgfIkLpSxq"
+LAST_ORDER = "iFxcepkqmfLIjSg"
 BACKLOG = 0
-LEAD = 3
+LEAD = 2
 I_AHEAD = 1
 I_LAST = 1
-A_BUFS = 3
+A_BUFS = 2
 SHARE = 3
 X_DUE = 1
 X_LAST = 0
 X_TWO = 0
 G_SPLIT = 2
-GATE_BUFS = 6
+GATE_BUFS = 5
 ARG_BUFS = 4
 CODE_BUFS = 6
 UNIT_EARLY = 1
-M_BUFS = N_GROUPS
+RATE = 1
+Q_CALLS = 1
+M_BUFS = 8
 
 E_MAX = 1.0e8 - 1.0
 
@@ -134,13 +136,16 @@ def tile_slstmlayer_pa_t_kernel(
 
         def quantise_pair(s):
             g, half = divmod(s, GROUP_PAIRS)
-            for part in range(2):
-                cols = slice((part * GROUP_PAIRS + half) * PAIR_ROWS, (part * GROUP_PAIRS + half + 1) * PAIR_ROWS)
-                nc.vector.quantize_mx(
-                    out=ops[g]["codes"][:, cols].bitcast(FP8X4),
-                    scales=ops[g]["scales"][:, cols],
-                    in_=grouped_rows[s][:, part * 4 * PAIR_ROWS : (part + 1) * 4 * PAIR_ROWS],
-                )
+            if half == GROUP_PAIRS - 1:
+                n_calls = 2 if g == 0 else Q_CALLS
+                width = 2 * GROUP_ROWS // n_calls
+                for j in range(n_calls):
+                    cols = slice(j * width, (j + 1) * width)
+                    nc.vector.quantize_mx(
+                        out=ops[g]["codes"][:, cols].bitcast(FP8X4),
+                        scales=ops[g]["scales"][:, cols],
+                        in_=ops[g]["grouped"][:, j * 4 * width : (j + 1) * 4 * width],
+                    )
 
         def mx(out, lhs, lhs_cols, rhs, rhs_cols, start, stop):
             nc.tensor.matmul_mx(
@@ -156,7 +161,6 @@ def tile_slstmlayer_pa_t_kernel(
         weights = {}
         wbanks = {}
         ops = {}
-        grouped_rows = {}
         tr_banks = {}
         gates = {}
         f_banks = {}
@@ -181,15 +185,14 @@ def tile_slstmlayer_pa_t_kernel(
                 tr_banks[s, part] = transpose_rows(raw["xh"[part], g], half * PAIR_TILES, tag)
 
         def prep_copy(s, copies, parts=(0, 1)):
-            g = s // GROUP_PAIRS
+            g, half = divmod(s, GROUP_PAIRS)
             if g not in ops:
                 codes = codes_pool.tile([P, 2 * GROUP_ROWS], U32, tag="codes", name="codes", align_bytes=64)
                 scales = codes_pool.tile([P, 2 * GROUP_ROWS], U8, tag="scales", name="scales", align_bytes=64)
-                ops[g] = {"codes": codes, "scales": scales}
-            if s not in grouped_rows:
-                grouped_rows[s] = grouped_pool.tile([P, 8 * PAIR_ROWS], BF16, tag="act_grouped", name="grouped", align_bytes=64)
+                grouped = grouped_pool.tile([P, 8 * GROUP_ROWS], BF16, tag="act_grouped", name="grouped", align_bytes=64)
+                ops[g] = {"codes": codes, "scales": scales, "grouped": grouped}
             for part in parts:
-                copy_out(grouped_rows[s], part, tr_banks[s, part], copies[part])
+                copy_out(ops[g]["grouped"], part * GROUP_PAIRS + half, tr_banks[s, part], copies[part])
 
         def f_T(s, tag="pf"):
             g, half = divmod(s, GROUP_PAIRS)
@@ -213,9 +216,8 @@ def tile_slstmlayer_pa_t_kernel(
 
         def f_clamp(s):
             g, half = divmod(s, GROUP_PAIRS)
-            for c in (2 * half, 2 * half + 1):
-                flat = gates[g][:, c, :]
-                nc.gpsimd.tensor_scalar(out=flat, in0=flat, scalar1=E_MAX, scalar2=0.0, op0=ALU.min, op1=ALU.max)
+            both = gates[g][:, 2 * half : 2 * half + 2, :].rearrange("p c r -> p (c r)")
+            nc.gpsimd.tensor_scalar(out=both, in0=both, scalar1=E_MAX, scalar2=0.0, op0=ALU.min, op1=ALU.max)
 
         def f_log(s):
             g, half = divmod(s, GROUP_PAIRS)
@@ -358,6 +360,7 @@ def tile_slstmlayer_pa_t_kernel(
 
         keep_warm(3)
         prep_T(0, (0,))
+        keep_warm(1)
         weight_T(wfx_raw, "fx", "pi")
         prep_T(0, (1,))
         weight_T(wfh_raw, "fh", "ps")
@@ -367,6 +370,7 @@ def tile_slstmlayer_pa_t_kernel(
         prep_copy(0, (V, A), (1,))
         weight_copy("fh", (V, A))
         quantise(weights["fx"])
+        keep_warm(1)
         prep_T(1, (1,))
         prep_copy(1, (V, A), (0,))
         quantise_pair(0)
@@ -377,9 +381,11 @@ def tile_slstmlayer_pa_t_kernel(
         nc.tensor.transpose(bias_bank[:], bias_rows[:], ident_bf16[:])
         neg_bf = consts.tile([P, CHUNKS], F32, tag="neg_bf")
         nc.vector.tensor_scalar(out=neg_bf[:], in0=bias_bank[:, 0:CHUNKS], scalar1=-1.0, scalar2=None, op0=ALU.mult)
+        keep_warm(1)
         prep_T(2, (0,), tag="pi")
         prep_T(2, (1,), tag="pi")
         prep_copy(2, (V, A))
+        keep_warm(1)
         prep_T(3, (0,), tag="tr")
         prep_T(3, (1,), tag="tr")
         prep_copy(3, (V, A))
@@ -416,37 +422,32 @@ def tile_slstmlayer_pa_t_kernel(
         if S0_AT >= EXTRA:
             s_T(0)
 
-        todo = list(range(ROUNDS[0], N_PAIRS))
         quantised = set(range(ROUNDS[0] + EXTRA))
-        copied = set(quantised)
-        transposed = ROUNDS[0] + 3
         waiting = []
-        logged = ROUNDS[0]
         sent = 0
-        r = 1
+        unit_end = []
+        log_of = {}
+        first = ROUNDS[0]
+        for n in ROUNDS[1:]:
+            begin = len(unit_end)
+            steps = max(1, first - BACKLOG - begin)
+            for j in range(1, steps + 1):
+                unit_end.append(first + (-(-n * j // steps) if UNIT_EARLY else n * j // steps))
+            log_of[len(unit_end) - 1] = (first, n)
+            first += n
+        while len(unit_end) < N_PAIRS + 1:
+            unit_end.append(N_PAIRS)
+        last_log = max(log_of)
+        copied_end = ROUNDS[0] + EXTRA
         last_due = 0
+        r = 1
         for k in range(N_PAIRS):
+            due = k in log_of
             n = ROUNDS[r] if r < len(ROUNDS) else 0
-            log_step = max(0, logged - 1 - BACKLOG)
-            due = n > 0 and k >= log_step
-            left = logged + n - (todo[0] if todo else N_PAIRS)
-            steps_left = max(1, log_step - k + 1)
-            units = []
-            if n and k <= log_step:
-                count = left if due else -(-left // steps_left) if UNIT_EARLY else left // steps_left
-                units = todo[:count]
-                todo = todo[count:]
-            elif not n:
-                units = []
-            goal = min(N_PAIRS, (units[-1] if units else (todo[0] - 1 if todo else N_PAIRS - 1)) // GROUP_PAIRS * GROUP_PAIRS + GROUP_PAIRS)
-            preps = []
-            nxt = max(copied) + 1
-            want = max(goal, min(N_PAIRS, max(copied) + 2)) if todo or units else N_PAIRS
-            cap = min(N_PAIRS, (units[-1] if units else logged + n - 1) + 1 + LEAD + 2)
-            while nxt < min(want, max(cap, goal)):
-                preps.append(nxt)
-                copied.add(nxt)
-                nxt += 1
+            units = list(range(unit_end[k - 1] if k else ROUNDS[0], unit_end[k]))
+            goal = min(N_PAIRS, max((unit_end[k + 1] + 1) // 2 * 2, unit_end[k] + LEAD, copied_end + RATE))
+            preps = list(range(copied_end, goal))
+            copied_end = goal
             share = k < SHARE
             for a in LAST_ORDER if due else ORDER:
                 if a == "c":
@@ -510,9 +511,8 @@ def tile_slstmlayer_pa_t_kernel(
                         outs -= 1
                 elif a == "L":
                     if due:
-                        for s in range(logged, logged + n):
+                        for s in range(log_of[k][0], sum(log_of[k])):
                             f_log(s)
-                        logged += n
                         r += 1
                         last_due = k
         for s in range(sent, N_PAIRS):

@@ -28,7 +28,7 @@ N_PAIRS = BATCH // PAIR_ROWS
 ROUNDS = (4, 4, 4, 4)
 X_BUFS = 4
 HOLD = 1
-S_MODE = 0
+S_MODE = 2
 EXTRA = 2
 S0_AT = 1
 ORDER = "icFemgfIkLpSxq"
@@ -44,7 +44,7 @@ X_LAST = 0
 X_TWO = 0
 G_SPLIT = 2
 GATE_BUFS = 5
-ARG_BUFS = 4
+ARG_BUFS = 5
 CODE_BUFS = 6
 UNIT_EARLY = 1
 RATE = 1
@@ -244,6 +244,11 @@ def tile_slstmlayer_pa_t_kernel(
                     out=s_banks[s][t][:], lhsT=neg_ident[:], rhs=raw["m", g][:, half * PAIR_TILES + t, :], start=False, stop=True
                 )
 
+            if S_MODE == 2:
+                for t, bank in enumerate(s_banks[s]):
+                    nc.tensor.matmul(
+                        out=bank[:], lhsT=neg_ident[:], rhs=raw["m", g][:, half * PAIR_TILES + t, :], start=True, stop=False
+                    )
             for t, bank in enumerate(s_banks[s]):
                 for c in range(CHUNKS):
                     nc.tensor.matmul(
@@ -251,8 +256,8 @@ def tile_slstmlayer_pa_t_kernel(
                         lhsT=gates[g][:, c, (half * PAIR_TILES + t) * P : (half * PAIR_TILES + t + 1) * P],
                         rhs=ident_f32[:],
                         is_transpose=True,
-                        start=(c == 0),
-                        stop=False,
+                        start=(c == 0 and S_MODE != 2),
+                        stop=(c == CHUNKS - 1 and S_MODE == 2),
                     )
                 if S_MODE == 0:
                     minus_m(t)

@@ -32,7 +32,7 @@ S_MODE = 2
 EXTRA = 2
 S0_AT = 1
 ORDER = "icFemgfIkLpSxq"
-LAST_ORDER = "iFxcepkqmfLIjSg"
+LAST_ORDER = "iFxcepkqmfLIwjSg"
 BACKLOG = 0
 LEAD = 2
 I_AHEAD = 1
@@ -48,6 +48,11 @@ ARG_BUFS = 5
 CODE_BUFS = 6
 UNIT_EARLY = 1
 RATE = 1
+WARM = 2
+WARM0 = 2
+X_SELF = 0
+FINAL_ORDER = "iFxcepkqmfLIwjSg"
+HW = (1, 0, 0, 1, 1, 1)
 Q_CALLS = 1
 M_BUFS = 8
 
@@ -365,17 +370,19 @@ def tile_slstmlayer_pa_t_kernel(
 
         keep_warm(3)
         prep_T(0, (0,))
-        keep_warm(1)
+        keep_warm(HW[0])
         weight_T(wfx_raw, "fx", "pi")
+        keep_warm(HW[1])
         prep_T(0, (1,))
         weight_T(wfh_raw, "fh", "ps")
+        keep_warm(HW[2])
         prep_copy(0, (V, A), (0,))
         weight_copy("fx", (A, V))
         prep_T(1, (0,))
         prep_copy(0, (V, A), (1,))
         weight_copy("fh", (V, A))
         quantise(weights["fx"])
-        keep_warm(1)
+        keep_warm(HW[3])
         prep_T(1, (1,))
         prep_copy(1, (V, A), (0,))
         quantise_pair(0)
@@ -386,11 +393,11 @@ def tile_slstmlayer_pa_t_kernel(
         nc.tensor.transpose(bias_bank[:], bias_rows[:], ident_bf16[:])
         neg_bf = consts.tile([P, CHUNKS], F32, tag="neg_bf")
         nc.vector.tensor_scalar(out=neg_bf[:], in0=bias_bank[:, 0:CHUNKS], scalar1=-1.0, scalar2=None, op0=ALU.mult)
-        keep_warm(1)
+        keep_warm(HW[4])
         prep_T(2, (0,), tag="pi")
         prep_T(2, (1,), tag="pi")
         prep_copy(2, (V, A))
-        keep_warm(1)
+        keep_warm(HW[5])
         prep_T(3, (0,), tag="tr")
         prep_T(3, (1,), tag="tr")
         prep_copy(3, (V, A))
@@ -419,6 +426,7 @@ def tile_slstmlayer_pa_t_kernel(
         for s in range(ROUNDS[0], ROUNDS[0] + EXTRA):
             prep_copy(s, (V, V))
             if s == ROUNDS[0] + S0_AT:
+                keep_warm(WARM0)
                 s_T(0)
             prep_T(s + 1)
             if s % GROUP_PAIRS == 0:
@@ -454,7 +462,7 @@ def tile_slstmlayer_pa_t_kernel(
             preps = list(range(copied_end, goal))
             copied_end = goal
             share = k < SHARE
-            for a in LAST_ORDER if due else ORDER:
+            for a in FINAL_ORDER if k == last_log else LAST_ORDER if due else ORDER:
                 if a == "c":
                     for s in preps:
                         prep_copy(s, (V, A if share else V))
@@ -481,7 +489,7 @@ def tile_slstmlayer_pa_t_kernel(
                     if k + 1 < N_PAIRS and k + 1 not in i_banks:
                         i_T(k + 1)
                 elif a == "j":
-                    for s in range(k + 1, min(N_PAIRS, k + 1 + (I_AHEAD if r < len(ROUNDS) - 1 else I_LAST))):
+                    for s in range(k + 1, min(N_PAIRS, k + 1 + (I_LAST if k == last_log else I_AHEAD))):
                         if s not in a_tiles:
                             chain_i(s)
                             if s + 1 < N_PAIRS:
@@ -492,6 +500,8 @@ def tile_slstmlayer_pa_t_kernel(
                     chain_g(k)
                 elif a == "f":
                     chain_f(k)
+                elif a == "w":
+                    keep_warm(WARM)
                 elif a == "S":
                     if k + 1 < N_PAIRS:
                         s_T(k + 1)
@@ -510,7 +520,9 @@ def tile_slstmlayer_pa_t_kernel(
                         f_clamp(units[0])
                 elif a == "x":
                     outs = X_LAST if due and r == len(ROUNDS) - 1 else 0 if due and not X_DUE else (2 if k >= N_PAIRS - ROUNDS[-1] + HOLD else 0) if not n else 2 if r > 1 and k <= last_due + X_TWO else 1
-                    while outs and sent < k:
+                    if k == last_log:
+                        outs = X_LAST
+                    while outs and sent < (k + 1 if k == last_log and X_SELF else k):
                         exponentials(sent)
                         sent += 1
                         outs -= 1

@@ -130,8 +130,8 @@ def tile_slstmlayer_pa_t_kernel(
 
         def new_operand(pool, name):
             grouped = grouped_pool.tile([P, 8 * PAIR_ROWS], BF16, tag="w_grouped", name="grouped", align_bytes=64)
-            codes = pool.tile([P, 2 * PAIR_ROWS], U32, tag=name + "_codes", name="codes", align_bytes=64)
-            scales = pool.tile([P, 2 * PAIR_ROWS], U8, tag=name + "_scales", name="scales", align_bytes=64)
+            codes = pool.tile([P, 2 * PAIR_ROWS], U32, tag=name + "_codes", name="codes", align_bytes=256)
+            scales = pool.tile([P, 2 * PAIR_ROWS], U8, tag=name + "_scales", name="scales", align_bytes=256)
             return {"grouped": grouped, "codes": codes, "scales": scales}
 
         def quantise(op):
@@ -192,8 +192,8 @@ def tile_slstmlayer_pa_t_kernel(
         def prep_copy(s, copies, parts=(0, 1)):
             g, half = divmod(s, GROUP_PAIRS)
             if g not in ops:
-                codes = codes_pool.tile([P, 2 * GROUP_ROWS], U32, tag="codes", name="codes", align_bytes=64)
-                scales = codes_pool.tile([P, 2 * GROUP_ROWS], U8, tag="scales", name="scales", align_bytes=64)
+                codes = codes_pool.tile([P, 2 * GROUP_ROWS], U32, tag="codes", name="codes", align_bytes=256)
+                scales = codes_pool.tile([P, 2 * GROUP_ROWS], U8, tag="scales", name="scales", align_bytes=256)
                 grouped = grouped_pool.tile([P, 8 * GROUP_ROWS], BF16, tag="act_grouped", name="grouped", align_bytes=64)
                 ops[g] = {"codes": codes, "scales": scales, "grouped": grouped}
             for part in parts:

from contextlib import ExitStack

import concourse.mybir as mybir
from concourse.masks import make_identity

F32 = mybir.dt.float32
BF16 = mybir.dt.bfloat16
U32 = mybir.dt.uint32
U8 = mybir.dt.uint8
FP8X4 = mybir.dt.float8_e4m3fn_x4
ACT = mybir.ActivationFunctionType
ALU = mybir.AluOpType

P = 128
BATCH = 4096
FEAT = 512
HID = 512
WORDS = FEAT // 2
CHUNKS = HID // P

PAIR_TILES = 2
PAIR_ROWS = PAIR_TILES * P
GROUP_PAIRS = 2
GROUP_TILES = GROUP_PAIRS * PAIR_TILES
GROUP_ROWS = GROUP_TILES * P
N_GROUPS = BATCH // GROUP_ROWS
N_PAIRS = BATCH // PAIR_ROWS
ROUNDS = (4, 4, 4, 4)
X_BUFS = 4
HOLD = 1
S_MODE = 2
EXTRA = 2
S0_AT = 1
ORDER = "icFemgfIkLpSxq"
LAST_ORDER = "iFxcepkqmfLIwjSg"
BACKLOG = 0
LEAD = 2
I_AHEAD = 1
I_LAST = 1
A_BUFS = 2
SHARE = 3
X_DUE = 1
X_LAST = 0
X_TWO = 0
G_SPLIT = 2
GATE_BUFS = 5
ARG_BUFS = 5
CODE_BUFS = 6
UNIT_EARLY = 1
RATE = 1
WARM = 2
WARM0 = 2
X_SELF = 0
FINAL_ORDER = "iFxcepkqmfLIwjSg"
HW = (1, 0, 0, 1, 1, 1)
Q_CALLS = 1
M_BUFS = 8

E_MAX = 1.0e8 - 1.0


FLOPS = 2 * BATCH * HID * FEAT * 4


def tile_slstmlayer_pa_t_kernel(
    tc, x, h_prev, m_prev, Wi_x, b_i, Wi_h, Wf_x, b_f, Wf_h, out_0, out_1, out_2
):
    nc = tc.nc
    with ExitStack() as ctx:
        consts = ctx.enter_context(tc.tile_pool(name="consts", bufs=1))
        raws = ctx.enter_context(tc.tile_pool(name="raws", bufs=5))
        grouped_pool = ctx.enter_context(tc.tile_pool(name="grouped_pool", bufs=2))
        codes_pool = ctx.enter_context(tc.tile_pool(name="codes_pool", bufs=CODE_BUFS))
        gate_pool = ctx.enter_context(tc.tile_pool(name="gate_pool", bufs=GATE_BUFS))
        arg_pool = ctx.enter_context(tc.tile_pool(name="arg_pool", bufs=ARG_BUFS))
        a_pool = ctx.enter_context(tc.tile_pool(name="a_pool", bufs=A_BUFS))
        m_t_pool = ctx.enter_context(tc.tile_pool(name="m_t_pool", bufs=3))
        psum = ctx.enter_context(tc.psum_pool(name="psum", bufs=2))
        ctx.enter_context(tc.manual_schedule())

        idle_rows = consts.tile([P, HID], BF16, tag="idle_rows")
        nc.vector.memset(idle_rows[:], 0.0)
        ident_f32 = consts.tile([P, P], F32, tag="ident_f32")
        make_identity(nc, ident_f32[:])
        ident_bf16 = consts.tile([P, P], BF16, tag="ident_bf16")
        make_identity(nc, ident_bf16[:])

        def group_view(dram, g):
            rows = dram[g * GROUP_ROWS : (g + 1) * GROUP_ROWS, :]
            return rows.rearrange("(p t) k -> p t k", t=GROUP_TILES)

        def pair_view(dram, s):
            g, half = divmod(s, GROUP_PAIRS)
            return group_view(dram, g)[:, half * PAIR_TILES : (half + 1) * PAIR_TILES, :]

        raw = {}

        def new_raw(name, g):
            raw[name, g] = raws.tile([P, GROUP_TILES, FEAT], BF16, tag=name, name=name, bufs=M_BUFS if name == "m" else X_BUFS)

        def load_group(name, dram, g):
            new_raw(name, g)
            nc.sync.dma_start(out=raw[name, g][:], in_=group_view(dram, g))

        def load_pair(name, dram, s):
            g, half = divmod(s, GROUP_PAIRS)
            nc.sync.dma_start(
                out=raw[name, g][:, half * PAIR_TILES : (half + 1) * PAIR_TILES, :], in_=pair_view(dram, s)
            )

        def load_weight(w, name):
            tile = arg_pool.tile([P, CHUNKS, FEAT], BF16, tag="args", name=name)
            nc.sync.dma_start(out=tile[:], in_=w.rearrange("(c p) k -> p c k", p=P))
            return tile

        def transpose_rows(rows, first_tile, tag):
            words = rows[:].rearrange("p t k -> p (t k)").bitcast(F32)
            bank = psum.tile([P, 2, PAIR_ROWS], F32, tag=tag, name="word_bank")
            for t in range(PAIR_TILES):
                row = (first_tile + t) * WORDS
                for u in range(2):
                    nc.tensor.transpose(
                        bank[:, u, t * P : (t + 1) * P], words[:, row + u : row + WORDS : 2], ident_f32[:]
                    )
            return bank

        def copy_out(grouped, part, bank, copy):
            words = grouped[:].bitcast(F32)[:, part * 2 * PAIR_ROWS : (part + 1) * 2 * PAIR_ROWS]
            copy(out=words.rearrange("p (r u) -> p r u", u=2), in_=bank[:].rearrange("p u r -> p r u"))

        def new_operand(pool, name):
            grouped = grouped_pool.tile([P, 8 * PAIR_ROWS], BF16, tag="w_grouped", name="grouped", align_bytes=64)
            codes = pool.tile([P, 2 * PAIR_ROWS], U32, tag=name + "_codes", name="codes", align_bytes=256)
            scales = pool.tile([P, 2 * PAIR_ROWS], U8, tag=name + "_scales", name="scales", align_bytes=256)
            return {"grouped": grouped, "codes": codes, "scales": scales}

        def quantise(op):
            nc.vector.quantize_mx(
                out=op["codes"][:].bitcast(FP8X4), scales=op["scales"][:], in_=op["grouped"][:]
            )

        def quantise_pair(s):
            g, half = divmod(s, GROUP_PAIRS)
            if half == GROUP_PAIRS - 1:
                n_calls = 2 if g == 0 else Q_CALLS
                width = 2 * GROUP_ROWS // n_calls
                for j in range(n_calls):
                    cols = slice(j * width, (j + 1) * width)
                    nc.vector.quantize_mx(
                        out=ops[g]["codes"][:, cols].bitcast(FP8X4),
                        scales=ops[g]["scales"][:, cols],
                        in_=ops[g]["grouped"][:, j * 4 * width : (j + 1) * 4 * width],
                    )

        def mx(out, lhs, lhs_cols, rhs, rhs_cols, start, stop):
            nc.tensor.matmul_mx(
                out=out,
                lhsT=lhs["codes"][:, lhs_cols].bitcast(FP8X4),
                lhsT_scale=lhs["scales"][:, lhs_cols],
                rhs=rhs["codes"][:, rhs_cols].bitcast(FP8X4),
                rhs_scale=rhs["scales"][:, rhs_cols],
                start=start,
                stop=stop,
            )

        weights = {}
        wbanks = {}
        ops = {}
        tr_banks = {}
        gates = {}
        f_banks = {}
        i_banks = {}
        s_banks = {}
        args = {}
        X_COLS = slice(0, GROUP_ROWS)
        H_COLS = slice(GROUP_ROWS, 2 * GROUP_ROWS)

        def weight_T(rows, name, tags):
            wbanks[name] = [transpose_rows(rows, 0, tags), transpose_rows(rows, PAIR_TILES, tags)]

        def weight_copy(name, copies, parts=(0, 1)):
            if name not in weights:
                weights[name] = new_operand(consts, name)
            for part in parts:
                copy_out(weights[name]["grouped"], part, wbanks[name][part], copies[part])

        def prep_T(s, parts=(0, 1), tag="tr"):
            g, half = divmod(s, GROUP_PAIRS)
            for part in parts:
                tr_banks[s, part] = transpose_rows(raw["xh"[part], g], half * PAIR_TILES, tag)

        def prep_copy(s, copies, parts=(0, 1)):
            g, half = divmod(s, GROUP_PAIRS)
            if g not in ops:
                codes = codes_pool.tile([P, 2 * GROUP_ROWS], U32, tag="codes", name="codes", align_bytes=256)
                scales = codes_pool.tile([P, 2 * GROUP_ROWS], U8, tag="scales", name="scales", align_bytes=256)
                grouped = grouped_pool.tile([P, 8 * GROUP_ROWS], BF16, tag="act_grouped", name="grouped", align_bytes=64)
                ops[g] = {"codes": codes, "scales": scales, "grouped": grouped}
            for part in parts:
                copy_out(ops[g]["grouped"], part * GROUP_PAIRS + half, tr_banks[s, part], copies[part])

        def f_T(s, tag="pf"):
            g, half = divmod(s, GROUP_PAIRS)
            f_banks[s] = []
            for c in (2 * half, 2 * half + 1):
                bank = psum.tile([P, GROUP_ROWS], F32, tag=tag, name="f_bank")
                cols = slice(c * P, (c + 1) * P)
                mx(bank[:], weights["fx"], cols, ops[g], X_COLS, True, False)
                mx(bank[:], weights["fh"], cols, ops[g], H_COLS, False, True)
                f_banks[s].append(bank)

        def f_exp(s):
            g, half = divmod(s, GROUP_PAIRS)
            if half == 0:
                gates[g] = gate_pool.tile([P, CHUNKS, GROUP_ROWS], F32, tag="gate", name="gate")
            for j, bank in enumerate(f_banks[s]):
                c = 2 * half + j
                nc.scalar.activation(
                    out=gates[g][:, c, :], in_=bank[:], func=ACT.Exp, bias=neg_bf[:, c : c + 1], scale=-1.0
                )

        def f_clamp(s):
            g, half = divmod(s, GROUP_PAIRS)
            both = gates[g][:, 2 * half : 2 * half + 2, :].rearrange("p c r -> p (c r)")
            nc.gpsimd.tensor_scalar(out=both, in0=both, scalar1=E_MAX, scalar2=0.0, op0=ALU.min, op1=ALU.max)

        def f_log(s):
            g, half = divmod(s, GROUP_PAIRS)
            rows = gates[g][:, :, half * PAIR_ROWS : (half + 1) * PAIR_ROWS]
            nc.scalar.activation(out=rows, in_=rows, func=ACT.Ln, bias=one[:], scale=1.0)

        def i_T(s):
            g, half = divmod(s, GROUP_PAIRS)
            i_banks[s] = []
            for t in range(PAIR_TILES):
                bank = psum.tile([P, HID], F32, tag="pi", name="i_bank")
                row = half * PAIR_ROWS + t * P
                mx(bank[:], ops[g], slice(row, row + P), weights["ix"], slice(0, HID), True, False)
                row += GROUP_ROWS
                mx(bank[:], ops[g], slice(row, row + P), weights["ih"], slice(0, HID), False, True)
                i_banks[s].append(bank)

        def s_T(s):
            g, half = divmod(s, GROUP_PAIRS)
            s_banks[s] = [psum.tile([P, HID], F32, tag="ps", name="s_bank") for t in range(PAIR_TILES)]

            def minus_m(t):
                nc.tensor.matmul(
                    out=s_banks[s][t][:], lhsT=neg_ident[:], rhs=raw["m", g][:, half * PAIR_TILES + t, :], start=False, stop=True
                )

            if S_MODE == 2:
                for t, bank in enumerate(s_banks[s]):
                    nc.tensor.matmul(
                        out=bank[:], lhsT=neg_ident[:], rhs=raw["m", g][:, half * PAIR_TILES + t, :], start=True, stop=False
                    )
            for t, bank in enumerate(s_banks[s]):
                for c in range(CHUNKS):
                    nc.tensor.matmul(
                        out=bank[:, c * P : (c + 1) * P],
                        lhsT=gates[g][:, c, (half * PAIR_TILES + t) * P : (half * PAIR_TILES + t + 1) * P],
                        rhs=ident_f32[:],
                        is_transpose=True,
                        start=(c == 0 and S_MODE != 2),
                        stop=(c == CHUNKS - 1 and S_MODE == 2),
                    )
                if S_MODE == 0:
                    minus_m(t)
            if S_MODE == 1:
                for t in range(PAIR_TILES):
                    minus_m(t)

        m_ts = {}
        a_tiles = {}

        def chain_i(s):
            a_tiles[s] = a_pool.tile([P, PAIR_TILES * HID], F32, tag="a_tile", name="a_tile")
            for t in range(PAIR_TILES):
                cols = slice(t * HID, (t + 1) * HID)
                nc.vector.tensor_tensor(out=a_tiles[s][:, cols], in0=i_banks[s][t][:], in1=bi_all[:], op=ALU.add)

        def chain_m(s):
            args[s] = arg_pool.tile([P, 2, PAIR_TILES * HID], F32, tag="args", name="args")
            m_ts[s] = m_t_pool.tile([P, PAIR_TILES * HID], F32, tag="m_t", name="m_t")
            for t in range(PAIR_TILES):
                cols = slice(t * HID, (t + 1) * HID)
                nc.vector.scalar_tensor_tensor(
                    out=m_ts[s][:, cols], in0=s_banks[s][t][:], scalar=-1.0, in1=a_tiles[s][:, cols], op0=ALU.mult, op1=ALU.max
                )
            nc.sync.dma_start(out=pair_view(out_0, s), in_=m_ts[s][:].rearrange("p (t k) -> p t k", t=PAIR_TILES))

        def chain_g(s):
            for j in range(G_SPLIT):
                cols = slice(j * PAIR_TILES * HID // G_SPLIT, (j + 1) * PAIR_TILES * HID // G_SPLIT)
                nc.gpsimd.tensor_tensor(out=args[s][:, 0, cols], in0=a_tiles[s][:, cols], in1=m_ts[s][:, cols], op=ALU.subtract)

        def chain_f(s):
            for t in range(PAIR_TILES):
                cols = slice(t * HID, (t + 1) * HID)
                nc.vector.scalar_tensor_tensor(
                    out=args[s][:, 1, cols], in0=s_banks[s][t][:], scalar=-1.0, in1=m_ts[s][:, cols], op0=ALU.mult, op1=ALU.subtract
                )

        def exponentials(s):
            both = args[s][:].rearrange("p a w -> p (a w)")
            nc.scalar.activation(out=both, in_=both, func=ACT.Exp)
            nc.sync.dma_start(out=pair_view(out_1, s), in_=args[s][:, 0, :].rearrange("p (t k) -> p t k", t=PAIR_TILES))
            nc.sync.dma_start(out=pair_view(out_2, s), in_=args[s][:, 1, :].rearrange("p (t k) -> p t k", t=PAIR_TILES))

        V = nc.vector.tensor_copy
        A = nc.scalar.copy

        bias_rows = consts.tile([P, P], BF16, tag="bias_rows")
        nc.vector.memset(bias_rows[:], 0.0)
        nc.scalar.dma_start(out=bias_rows[0:CHUNKS, :], in_=b_f.rearrange("(c p) -> c p", p=P))
        bi_row = consts.tile([P, HID], BF16, tag="bi_row")
        nc.vector.memset(bi_row[:], 0.0)
        nc.scalar.dma_start(out=bi_row[0:1, :], in_=b_i.rearrange("(a k) -> a k", a=1))
        ones = consts.tile([P, P], BF16, tag="ones")
        nc.vector.memset(ones[:], 1.0)
        one = consts.tile([P, 1], F32, tag="one")
        nc.vector.memset(one[:], 1.0)
        warm = consts.tile([P, 1], F32, tag="warm")
        nc.scalar.activation(out=warm[:], in_=one[:], func=ACT.Exp)
        neg_ident = consts.tile([P, P], BF16, tag="neg_ident")
        nc.vector.tensor_scalar(out=neg_ident[:], in0=ident_bf16[:], scalar1=-1.0, scalar2=None, op0=ALU.mult)

        new_raw("x", 0)
        new_raw("h", 0)
        load_pair("x", x, 0)
        wfx_raw = load_weight(Wf_x, "wfx_raw")
        load_pair("h", h_prev, 0)
        wfh_raw = load_weight(Wf_h, "wfh_raw")
        load_pair("x", x, 1)
        load_pair("h", h_prev, 1)
        load_group("x", x, 1)
        load_group("h", h_prev, 1)
        wix_raw = load_weight(Wi_x, "wix_raw")
        wih_raw = load_weight(Wi_h, "wih_raw")
        load_group("x", x, 2)
        load_group("h", h_prev, 2)
        load_group("m", m_prev, 0)
        load_group("x", x, 3)
        load_group("h", h_prev, 3)
        load_group("m", m_prev, 1)

        loaded = set()

        def load_activations(g):
            if g in loaded:
                return
            loaded.add(g)
            if g < N_GROUPS:
                load_group("x", x, g)
                load_group("h", h_prev, g)
                load_group("m", m_prev, g - 2)
            if g == N_GROUPS - 1:
                load_group("m", m_prev, g - 1)
                load_group("m", m_prev, g)

        def forget(s, tag="pf"):
            f_T(s, tag)
            f_exp(s)
            f_clamp(s)

        def keep_warm(count):
            for j in range(count):
                bank = psum.tile([P, HID], F32, tag="pf", name="idle_bank")
                nc.tensor.matmul(out=bank[:], lhsT=idle_rows[:, 0:P], rhs=idle_rows[:], start=True, stop=True)

        keep_warm(3)
        prep_T(0, (0,))
        keep_warm(HW[0])
        weight_T(wfx_raw, "fx", "pi")
        keep_warm(HW[1])
        prep_T(0, (1,))
        weight_T(wfh_raw, "fh", "ps")
        keep_warm(HW[2])
        prep_copy(0, (V, A), (0,))
        weight_copy("fx", (A, V))
        prep_T(1, (0,))
        prep_copy(0, (V, A), (1,))
        weight_copy("fh", (V, A))
        quantise(weights["fx"])
        keep_warm(HW[3])
        prep_T(1, (1,))
        prep_copy(1, (V, A), (0,))
        quantise_pair(0)
        quantise(weights["fh"])
        prep_copy(1, (V, A), (1,))
        quantise_pair(1)
        bias_bank = psum.tile([P, P], BF16, tag="pf", name="bias_bank")
        nc.tensor.transpose(bias_bank[:], bias_rows[:], ident_bf16[:])
        neg_bf = consts.tile([P, CHUNKS], F32, tag="neg_bf")
        nc.vector.tensor_scalar(out=neg_bf[:], in0=bias_bank[:, 0:CHUNKS], scalar1=-1.0, scalar2=None, op0=ALU.mult)
        keep_warm(HW[4])
        prep_T(2, (0,), tag="pi")
        prep_T(2, (1,), tag="pi")
        prep_copy(2, (V, A))
        keep_warm(HW[5])
        prep_T(3, (0,), tag="tr")
        prep_T(3, (1,), tag="tr")
        prep_copy(3, (V, A))
        forget(0)
        quantise_pair(2)
        quantise_pair(3)
        load_activations(X_BUFS)
        forget(1, "ps")
        load_activations(X_BUFS + 1)
        weight_T(wix_raw, "ix", "pi")
        forget(2)
        weight_T(wih_raw, "ih", "tr")
        forget(3, "ps")
        weight_copy("ix", (V, V))
        weight_copy("ih", (V, V))
        quantise(weights["ix"])
        bi_bank = psum.tile([P, HID], F32, tag="pi", name="bi_bank")
        nc.tensor.matmul(out=bi_bank[:], lhsT=ones[:], rhs=bi_row[:], start=True, stop=True)
        bi_all = consts.tile([P, HID], BF16, tag="bi_all")
        nc.scalar.copy(out=bi_all[:], in_=bi_bank[:])
        quantise(weights["ih"])
        prep_T(4)
        i_T(0)
        for s in range(ROUNDS[0]):
            f_log(s)
        for s in range(ROUNDS[0], ROUNDS[0] + EXTRA):
            prep_copy(s, (V, V))
            if s == ROUNDS[0] + S0_AT:
                keep_warm(WARM0)
                s_T(0)
            prep_T(s + 1)
            if s % GROUP_PAIRS == 0:
                load_activations(s // GROUP_PAIRS + X_BUFS)
            quantise_pair(s)
        if S0_AT >= EXTRA:
            s_T(0)

        quantised = set(range(ROUNDS[0] + EXTRA))
        waiting = []
        sent = 0
        unit_end = []
        log_of = {}
        first = ROUNDS[0]
        for n in ROUNDS[1:]:
            begin = len(unit_end)
            steps = max(1, first - BACKLOG - begin)
            for j in range(1, steps + 1):
                unit_end.append(first + (-(-n * j // steps) if UNIT_EARLY else n * j // steps))
            log_of[len(unit_end) - 1] = (first, n)
            first += n
        while len(unit_end) < N_PAIRS + 1:
            unit_end.append(N_PAIRS)
        last_log = max(log_of)
        copied_end = ROUNDS[0] + EXTRA
        last_due = 0
        r = 1
        for k in range(N_PAIRS):
            due = k in log_of
            n = ROUNDS[r] if r < len(ROUNDS) else 0
            units = list(range(unit_end[k - 1] if k else ROUNDS[0], unit_end[k]))
            goal = min(N_PAIRS, max((unit_end[k + 1] + 1) // 2 * 2, unit_end[k] + LEAD, copied_end + RATE))
            preps = list(range(copied_end, goal))
            copied_end = goal
            share = k < SHARE
            for a in FINAL_ORDER if k == last_log else LAST_ORDER if due else ORDER:
                if a == "c":
                    for s in preps:
                        prep_copy(s, (V, A if share else V))
                        waiting.append(s)
                        if s != preps[-1] and s + 1 < N_PAIRS:
                            prep_T(s + 1)
                            if s % GROUP_PAIRS == 0:
                                load_activations(s // GROUP_PAIRS + X_BUFS)
                elif a == "p":
                    for s in preps[-1:]:
                        if s + 1 < N_PAIRS:
                            prep_T(s + 1)
                            if s % GROUP_PAIRS == 0:
                                load_activations(s // GROUP_PAIRS + X_BUFS)
                elif a == "q":
                    for s in waiting:
                        quantise_pair(s)
                        quantised.add(s)
                    waiting = []
                elif a == "i":
                    if k not in a_tiles:
                        chain_i(k)
                elif a == "I":
                    if k + 1 < N_PAIRS and k + 1 not in i_banks:
                        i_T(k + 1)
                elif a == "j":
                    for s in range(k + 1, min(N_PAIRS, k + 1 + (I_LAST if k == last_log else I_AHEAD))):
                        if s not in a_tiles:
                            chain_i(s)
                            if s + 1 < N_PAIRS:
                                i_T(s + 1)
                elif a == "m":
                    chain_m(k)
                elif a == "g":
                    chain_g(k)
                elif a == "f":
                    chain_f(k)
                elif a == "w":
                    keep_warm(WARM)
                elif a == "S":
                    if k + 1 < N_PAIRS:
                        s_T(k + 1)
                elif a == "F":
                    for s in units:
                        assert s | 1 in quantised and s & ~1 in quantised
                        f_T(s)
                        if len(units) > 1:
                            f_exp(s)
                            f_clamp(s)
                elif a == "e":
                    if len(units) == 1:
                        f_exp(units[0])
                elif a == "k":
                    if len(units) == 1:
                        f_clamp(units[0])
                elif a == "x":
                    outs = X_LAST if due and r == len(ROUNDS) - 1 else 0 if due and not X_DUE else (2 if k >= N_PAIRS - ROUNDS[-1] + HOLD else 0) if not n else 2 if r > 1 and k <= last_due + X_TWO else 1
                    if k == last_log:
                        outs = X_LAST
                    while outs and sent < (k + 1 if k == last_log and X_SELF else k):
                        exponentials(sent)
                        sent += 1
                        outs -= 1
                elif a == "L":
                    if due:
                        for s in range(log_of[k][0], sum(log_of[k])):
                            f_log(s)
                        r += 1
                        last_due = k
        for s in range(sent, N_PAIRS):
            exponentials(s)
